import numpy as np
import ml_dtypes


def mxq(x, axis, fmt="e4m3"):
    dtype, down = {"e4m3": (ml_dtypes.float8_e4m3fn, 7), "e5m2": (ml_dtypes.float8_e5m2, 14)}[fmt]
    v = np.moveaxis(np.asarray(x, np.float32).astype(ml_dtypes.bfloat16).astype(np.float64), axis, -1)
    blocks = v.reshape(v.shape[:-1] + (-1, 32))
    amax = np.abs(blocks).max(-1, keepdims=True)
    byte = np.maximum(np.where(amax > 0, np.frexp(amax)[1] - 1 + 127, 0) - down, 1)
    scale = np.exp2(byte - 127.0)
    codes = (blocks / scale).astype(np.float32).astype(dtype).astype(np.float64)
    return np.moveaxis((codes * scale).reshape(v.shape), -1, axis)


WIDE = False


def mx_kscale(k):
    if not WIDE:
        return np.ones(k)
    levels = np.array([10, -10, 5, -5, 0])
    a = np.random.permutation(np.resize(levels, k // 512 * 4)).reshape(k // 512, 4)
    idx = np.arange(k)
    return np.exp2(a[idx // 512, idx % 128 // 32])


BF16 = ml_dtypes.bfloat16


def bf(x):
    return np.asarray(x, np.float32).astype(BF16)


def f64(x):
    return np.asarray(x).astype(np.float64)


E2M1 = np.array([0.0, 0.5, 1.0, 1.5, 2.0, 3.0, 4.0, 6.0, -0.0, -0.5, -1.0, -1.5, -2.0, -3.0, -4.0, -6.0])


def pack_weight(w, fmt):
    k, n = w.shape
    w = f64(bf(w)).reshape(k // 32, 32, n)
    amax = np.abs(w).max(1)
    if fmt == "e4m3":
        byte = np.frexp(amax)[1] - 1 + 127 - 7
    else:
        mant, ex = np.frexp(amax / 6.0)
        byte = np.where(mant > 0.5, ex, ex - 1) + 127
    byte = np.clip(np.where(amax > 0, byte, 1), 1, 254)
    scaled = (w * np.exp2(127.0 - byte)[:, None, :]).reshape(k, n).astype(np.float32)
    by_word = np.ascontiguousarray(scaled.reshape(k // 512, 128, 4, n).transpose(0, 1, 3, 2))
    if fmt == "e4m3":
        words = by_word.astype(ml_dtypes.float8_e4m3fn).view(np.uint8)
    else:
        c = by_word.astype(ml_dtypes.float4_e2m1fn).view(np.uint8) & 0xF
        words = c[..., 0::2] | (c[..., 1::2] << 4)
    return np.ascontiguousarray(words), np.ascontiguousarray(byte.astype(np.uint8).reshape(k // 512, 16, n))


def unpack_weight(words, scales, fmt):
    g, p, n, _ = words.shape
    if fmt == "e4m3":
        vals = np.ascontiguousarray(words).view(ml_dtypes.float8_e4m3fn).astype(np.float64)
    else:
        nib = np.empty((g, p, n, 4), np.uint8)
        nib[..., 0::2] = words & 0xF
        nib[..., 1::2] = words >> 4
        vals = E2M1[nib]
    vals = vals * np.repeat(np.exp2(scales.astype(np.float64) - 127.0), 8, axis=1)[..., None]
    return vals.transpose(0, 1, 3, 2).reshape(g * 512, n)


B, D, U = 512, 1024, 1024


def hard_sigmoid(v):
    return np.clip(0.2 * v + 0.5, 0.0, 1.0)


def setup_inputs():
    s = mx_kscale(D)
    inputs = bf(np.random.standard_normal((B, D)) * s)
    h_tm1 = bf(np.random.standard_normal((B, U)))
    kernel_words, kernel_scales = pack_weight(np.random.standard_normal((D, 3 * U)) * 0.64 / np.sqrt(D) / s[:, None], "e4m3")
    recurrent_kernel_words, recurrent_kernel_scales = pack_weight(np.random.standard_normal((U, 3 * U)) * 0.64 / np.sqrt(U), "e4m3")
    bias = bf(np.random.standard_normal((2, 3 * U)) * 0.2)
    return {"inputs": inputs,
            "h_tm1": h_tm1,
            "kernel_words": kernel_words,
            "kernel_scales": kernel_scales,
            "recurrent_kernel_words": recurrent_kernel_words,
            "recurrent_kernel_scales": recurrent_kernel_scales,
            "bias": bias}


def reference(inputs, h_tm1, kernel_words, kernel_scales, recurrent_kernel_words, recurrent_kernel_scales, bias):
    kernel_q = unpack_weight(kernel_words, kernel_scales, "e4m3")
    recurrent_kernel_q = unpack_weight(recurrent_kernel_words, recurrent_kernel_scales, "e4m3")
    units = recurrent_kernel_q.shape[0]
    h_prev = f64(h_tm1)
    b = f64(bias)
    input_bias, recurrent_bias = b[0], b[1]

    matrix_x = (mxq(f64(inputs), 1, "e4m3") @ kernel_q) + input_bias
    x_z, x_r, x_h = np.split(matrix_x, 3, axis=-1)

    matrix_inner = (mxq(h_prev, 1, "e4m3") @ recurrent_kernel_q) + recurrent_bias
    rec_z = matrix_inner[:, :units]
    rec_r = matrix_inner[:, units:2 * units]
    rec_h = matrix_inner[:, 2 * units:]

    z = hard_sigmoid(x_z + rec_z)
    r = hard_sigmoid(x_r + rec_r)
    hh = np.tanh(x_h + r * rec_h)
    h = z * h_prev + (1.0 - z) * hh
    return h

@@ -1,0 +1,271 @@
+from contextlib import ExitStack
+
+import concourse.mybir as mybir
+from concourse.masks import make_identity
+
+F32 = mybir.dt.float32
+BF16 = mybir.dt.bfloat16
+I32 = mybir.dt.int32
+U32 = mybir.dt.uint32
+U8 = mybir.dt.uint8
+FP8X4 = mybir.dt.float8_e4m3fn_x4
+ACT = mybir.ActivationFunctionType
+ALU = mybir.AluOpType
+
+P = 128
+PACK = 4
+K_PASS = P * PACK
+BATCH = 512
+DEPTH = 1024
+UNITS = 1024
+PASSES = DEPTH // K_PASS
+BATCH_TILES = BATCH // P
+UNIT_TILES = UNITS // P
+GATE_Z, GATE_R, GATE_H = 0, 1, 2
+FROM_X, FROM_H = 0, 1
+HALVES = 2
+F32_PER_PASS = K_PASS // 2
+ROW_LOADS = 2
+LOAD_TILES = 2
+LOAD_COLS = LOAD_TILES * P
+BANK = 512
+
+FLOPS = 2 * 2 * BATCH * DEPTH * 3 * UNITS
+
+
+def tile_gruskipcell_kernel(
+    tc, inputs, h_tm1, kernel_words, kernel_scales, recurrent_kernel_words, recurrent_kernel_scales, bias, out
+):
+    with ExitStack() as ctx:
+        gru_cell(
+            ctx, tc, inputs, h_tm1, kernel_words, kernel_scales, recurrent_kernel_words, recurrent_kernel_scales, bias, out
+        )
+
+
+def gru_cell(
+    ctx,
+    tc,
+    inputs,
+    h_tm1,
+    kernel_words,
+    kernel_scales,
+    recurrent_kernel_words,
+    recurrent_kernel_scales,
+    bias,
+    out,
+):
+    nc = tc.nc
+    ctx.enter_context(tc.manual_schedule())
+    consts = ctx.enter_context(tc.tile_pool(name="consts", bufs=1))
+    acts = ctx.enter_context(tc.tile_pool(name="acts", bufs=1))
+    weights = ctx.enter_context(tc.tile_pool(name="weights", bufs=1))
+    work = ctx.enter_context(tc.tile_pool(name="work", bufs=2))
+
+    w_planes = consts.tile([P, 3 * UNITS], U8, align_bytes=64)
+    nc.vector.memset(w_planes[:].bitcast(I32), 0)
+
+    ident_f32 = consts.tile([P, P], F32)
+    make_identity(nc, ident_f32[:])
+    ident_bf16 = consts.tile([P, P], BF16)
+    make_identity(nc, ident_bf16[:])
+
+    bias_rows = consts.tile([P, P], BF16)
+    nc.vector.memset(bias_rows[:], 0.0)
+    nc.scalar.dma_start(out=bias_rows[0 : 2 * 3 * UNIT_TILES, :], in_=bias.rearrange("b (c n) -> (b c) n", n=P))
+    z_bias_rows = consts.tile([P, UNITS], BF16)
+    nc.vector.memset(z_bias_rows[:], 0.0)
+    nc.scalar.dma_start(out=z_bias_rows[0:2, :], in_=bias[:, GATE_Z * UNITS : (GATE_Z + 1) * UNITS])
+    ones = consts.tile([P, P], BF16)
+    nc.vector.memset(ones[:], 1.0)
+
+    rows_dram = (inputs, h_tm1)
+    a_rows = []
+    for m in (FROM_X, FROM_H):
+        rows = acts.tile([P, BATCH_TILES, DEPTH], BF16, name="rows%d" % m)
+        a_rows.append(rows)
+        tiles = BATCH_TILES // ROW_LOADS
+        for i in range(ROW_LOADS):
+            nc.sync.dma_start(
+                out=rows[:, tiles * i : tiles * (i + 1), :],
+                in_=rows_dram[m][tiles * P * i : tiles * P * (i + 1), :].rearrange("(t b) k -> b t k", b=P),
+            )
+
+    scales_dram = (kernel_scales, recurrent_kernel_scales)
+    for quadrant in range(4):
+        for m in (FROM_X, FROM_H):
+            first = 32 * quadrant + 4 * PASSES * m
+            nc.sync.dma_start(
+                out=w_planes[first : first + 4 * PASSES, :].bitcast(I32),
+                in_=scales_dram[m].bitcast(I32)[:, 4 * quadrant : 4 * quadrant + 4, :],
+            )
+
+    words_dram = (kernel_words, recurrent_kernel_words)
+    w_words = {}
+    for load in range(UNIT_TILES // LOAD_TILES):
+        for m, gate in ((FROM_X, GATE_H), (FROM_X, GATE_R), (FROM_H, GATE_R), (FROM_H, GATE_H), (FROM_X, GATE_Z), (FROM_H, GATE_Z)):
+            words = weights.tile([P, PASSES, LOAD_COLS], U32, name="w%d_%d_%d" % (m, gate, load), align_bytes=64)
+            w_words[(m, gate, load)] = words
+            first = gate * UNITS + load * LOAD_COLS
+            nc.sync.dma_start(
+                out=words[:].bitcast(I32),
+                in_=words_dram[m]
+                .rearrange("g p n t -> g p (n t)")
+                .bitcast(I32)[:, :, first : first + LOAD_COLS]
+                .rearrange("g p n -> p g n"),
+            )
+
+    a_codes = []
+    a_scales = []
+    with tc.psum_pool(name="prep_psum", bufs=1) as prep_psum:
+
+        def transpose_and_quantise(m):
+            grouped = acts.tile([P, PASSES, BATCH, PACK], BF16, name="grouped%d" % m, align_bytes=64)
+            grouped_words = (
+                grouped[:]
+                .rearrange("p g c t -> p (g c t)")
+                .bitcast(F32)
+                .rearrange("p (g c u) -> p g c u", g=PASSES, u=HALVES)
+            )
+            for t in range(BATCH_TILES):
+                row_words = a_rows[m][:, t, :].bitcast(F32)
+                flipped = prep_psum.tile([P, PASSES, HALVES, P], F32, tag="flipped", bufs=4)
+                for g in range(PASSES):
+                    for u in range(HALVES):
+                        nc.tensor.transpose(
+                            flipped[:, g, u, :],
+                            row_words[:, F32_PER_PASS * g + u : F32_PER_PASS * (g + 1) : HALVES],
+                            ident_f32[:],
+                        )
+                copy = nc.vector.tensor_copy if t % 2 == 0 else nc.scalar.copy
+                copy(out=grouped_words[:, :, t * P : (t + 1) * P, :], in_=flipped[:].rearrange("p g u b -> p g b u"))
+            codes = acts.tile([P, PASSES, BATCH], U32, name="codes%d" % m, align_bytes=64)
+            scales = acts.tile([P, PASSES, BATCH], U8, name="scales%d" % m, align_bytes=64)
+            for g in range(PASSES):
+                nc.vector.quantize_mx(
+                    out=codes[:, g, :].bitcast(FP8X4),
+                    scales=scales[:, g, :],
+                    in_=grouped[:, g, :, :].rearrange("p c t -> p (c t)"),
+                )
+            a_codes.append(codes)
+            a_scales.append(scales)
+
+        transpose_and_quantise(FROM_X)
+
+        bias_cols_ps = prep_psum.tile([P, P], BF16)
+        nc.tensor.transpose(bias_cols_ps[:], bias_rows[:], ident_bf16[:])
+        bias_cols = consts.tile([P, 2, 3, UNIT_TILES], F32)
+        nc.vector.tensor_copy(
+            out=bias_cols[:].rearrange("p b c j -> p (b c j)"), in_=bias_cols_ps[:, 0 : 2 * 3 * UNIT_TILES]
+        )
+        r_bias = consts.tile([P, UNIT_TILES], F32)
+        nc.vector.tensor_tensor(out=r_bias[:], in0=bias_cols[:, 0, GATE_R, :], in1=bias_cols[:, 1, GATE_R, :], op=ALU.add)
+        nc.vector.tensor_scalar(out=r_bias[:], in0=r_bias[:], scalar1=0.2, scalar2=0.5, op0=ALU.mult, op1=ALU.add)
+        z_bias = consts.tile([P, UNITS], F32)
+        for c in range(UNITS // BANK):
+            z_bias_ps = prep_psum.tile([P, BANK], F32, bufs=2)
+            nc.tensor.matmul(z_bias_ps[:], lhsT=ones[:], rhs=z_bias_rows[:, c * BANK : (c + 1) * BANK], start=True, stop=True)
+            nc.vector.tensor_scalar(
+                out=z_bias[:, c * BANK : (c + 1) * BANK], in0=z_bias_ps[:], scalar1=0.2, scalar2=0.5, op0=ALU.mult, op1=ALU.add
+            )
+
+        transpose_and_quantise(FROM_H)
+
+    psum = ctx.enter_context(tc.psum_pool(name="psum", bufs=1, reuse_waits="tile"))
+
+    def weight_operand(m, gate, j, g):
+        load, inside = divmod(j, LOAD_TILES)
+        first_row = 4 * (PASSES * m + g)
+        first_col = gate * UNITS + j * P
+        return (
+            w_words[(m, gate, load)][:, g, inside * P : (inside + 1) * P].bitcast(FP8X4),
+            w_planes[first_row:P, first_col : first_col + P],
+        )
+
+    def units_by_batch(acc, gate, j, sources):
+        passes = [(m, g) for m in sources for g in range(PASSES)]
+        for i, (m, g) in enumerate(passes):
+            words, plane = weight_operand(m, gate, j, g)
+            nc.tensor.matmul_mx(
+                out=acc,
+                lhsT=words,
+                lhsT_scale=plane,
+                rhs=a_codes[m][:, g, :].bitcast(FP8X4),
+                rhs_scale=a_scales[m][:, g, :],
+                start=(i == 0),
+                stop=(i == len(passes) - 1),
+            )
+
+    def batch_by_units(acc, gate, j, sources):
+        passes = [(m, g) for m in sources for g in range(PASSES)]
+        for t in range(BATCH_TILES):
+            for i, (m, g) in enumerate(passes):
+                words, plane = weight_operand(m, gate, j, g)
+                nc.tensor.matmul_mx(
+                    out=acc[:, t, :],
+                    lhsT=a_codes[m][:, g, t * P : (t + 1) * P].bitcast(FP8X4),
+                    lhsT_scale=a_scales[m][:, g, t * P : (t + 1) * P],
+                    rhs=words,
+                    rhs_scale=plane,
+                    start=(i == 0),
+                    stop=(i == len(passes) - 1),
+                )
+
+    out_tiles = out.rearrange("(t b) n -> b t n", b=P)
+
+    def to_batch_by_units(cand):
+        cand_t = psum.tile([P, BATCH_TILES, P], F32, bufs=2)
+        for t in range(BATCH_TILES):
+            nc.tensor.transpose(cand_t[:, t, :], cand[:, t * P : (t + 1) * P], ident_f32[:])
+        return cand_t
+
+    def blend(j, cand_t, z_relu):
+        units = slice(j * P, (j + 1) * P)
+        diff = work.tile([P, BATCH_TILES, P], F32)
+        nc.vector.tensor_tensor(out=diff[:], in0=a_rows[FROM_H][:, :, units], in1=cand_t[:], op=ALU.subtract)
+        z_diff = work.tile([P, BATCH_TILES, P], F32)
+        nc.vector.scalar_tensor_tensor(out=z_diff[:], in0=z_relu[:], scalar=1.0, in1=diff[:], op0=ALU.min, op1=ALU.mult)
+        result = work.tile([P, BATCH_TILES, P], F32)
+        nc.vector.tensor_tensor(out=result[:], in0=z_diff[:], in1=cand_t[:], op=ALU.add)
+        nc.sync.dma_start(out=out_tiles[:, :, units], in_=result[:])
+
+    cand = None
+    z_relu = None
+    for j in range(UNIT_TILES):
+        acc_xh = psum.tile([P, BATCH], F32, bufs=2)
+        units_by_batch(acc_xh[:], GATE_H, j, (FROM_X,))
+        acc_r = psum.tile([P, BATCH], F32)
+        units_by_batch(acc_r[:], GATE_R, j, (FROM_X, FROM_H))
+        acc_rh = psum.tile([P, BATCH], F32)
+        units_by_batch(acc_rh[:], GATE_H, j, (FROM_H,))
+        acc_z = psum.tile([P, BATCH_TILES, P], F32, bufs=2)
+        batch_by_units(acc_z, GATE_Z, j, (FROM_X, FROM_H))
+        if j > 0:
+            cand_t = to_batch_by_units(cand)
+            z_before = z_relu
+
+        r_relu = work.tile([P, BATCH], F32)
+        nc.scalar.activation(out=r_relu[:], in_=acc_r[:], func=ACT.Relu, bias=r_bias[:, j : j + 1], scale=0.2)
+        rec_h = work.tile([P, BATCH], F32)
+        nc.scalar.activation(out=rec_h[:], in_=acc_rh[:], func=ACT.Identity, bias=bias_cols[:, 1, GATE_H, j : j + 1], scale=1.0)
+        gated = work.tile([P, BATCH], F32)
+        nc.vector.scalar_tensor_tensor(out=gated[:], in0=r_relu[:], scalar=1.0, in1=rec_h[:], op0=ALU.min, op1=ALU.mult)
+        pre_tanh = work.tile([P, BATCH], F32)
+        nc.vector.tensor_tensor(out=pre_tanh[:], in0=acc_xh[:], in1=gated[:], op=ALU.add)
+        cand = work.tile([P, BATCH], F32)
+        nc.scalar.activation(out=cand[:], in_=pre_tanh[:], func=ACT.Tanh, bias=bias_cols[:, 0, GATE_H, j : j + 1], scale=1.0)
+
+        z_line = work.tile([P, BATCH_TILES, P], F32)
+        nc.vector.scalar_tensor_tensor(
+            out=z_line[:],
+            in0=acc_z[:],
+            scalar=0.2,
+            in1=z_bias[:, j * P : (j + 1) * P].unsqueeze(1).to_broadcast([P, BATCH_TILES, P]),
+            op0=ALU.mult,
+            op1=ALU.add,
+        )
+        z_relu = work.tile([P, BATCH_TILES, P], F32)
+        nc.scalar.activation(out=z_relu[:], in_=z_line[:], func=ACT.Relu)
+
+        if j > 0:
+            blend(j - 1, cand_t, z_before)
+    blend(UNIT_TILES - 1, to_batch_by_units(cand), z_relu)

@@ -25,10 +25,12 @@ GATE_Z, GATE_R, GATE_H = 0, 1, 2
 FROM_X, FROM_H = 0, 1
 HALVES = 2
 F32_PER_PASS = K_PASS // 2
-ROW_LOADS = 2
-LOAD_TILES = 2
-LOAD_COLS = LOAD_TILES * P
 BANK = 512
+BANKS_PER_GATE = UNITS // BANK
+TILES_PER_BANK = BANK // P
+SCALE_ROWS = 4
+ROW_LOADS = (2, 4)
+Z_LAG = 2
 
 FLOPS = 2 * 2 * BATCH * DEPTH * 3 * UNITS
 
@@ -43,16 +45,7 @@ def tile_gruskipcell_kernel(
 
 
 def gru_cell(
-    ctx,
-    tc,
-    inputs,
-    h_tm1,
-    kernel_words,
-    kernel_scales,
-    recurrent_kernel_words,
-    recurrent_kernel_scales,
-    bias,
-    out,
+    ctx, tc, inputs, h_tm1, kernel_words, kernel_scales, recurrent_kernel_words, recurrent_kernel_scales, bias, out
 ):
     nc = tc.nc
     ctx.enter_context(tc.manual_schedule())
@@ -66,8 +59,6 @@ def gru_cell(
 
     ident_f32 = consts.tile([P, P], F32)
     make_identity(nc, ident_f32[:])
-    ident_bf16 = consts.tile([P, P], BF16)
-    make_identity(nc, ident_bf16[:])
 
     bias_rows = consts.tile([P, P], BF16)
     nc.vector.memset(bias_rows[:], 0.0)
@@ -77,48 +68,62 @@ def gru_cell(
     nc.scalar.dma_start(out=z_bias_rows[0:2, :], in_=bias[:, GATE_Z * UNITS : (GATE_Z + 1) * UNITS])
     ones = consts.tile([P, P], BF16)
     nc.vector.memset(ones[:], 1.0)
+    ident_bf16 = consts.tile([P, P], BF16)
+    make_identity(nc, ident_bf16[:])
 
     rows_dram = (inputs, h_tm1)
+    scales_dram = (kernel_scales, recurrent_kernel_scales)
+    words_dram = (kernel_words, recurrent_kernel_words)
     a_rows = []
-    for m in (FROM_X, FROM_H):
+    w_words = {}
+
+    def load_scales(m):
+        for quadrant in range(4):
+            first = 32 * quadrant + SCALE_ROWS * PASSES * m
+            nc.sync.dma_start(
+                out=w_planes[first : first + SCALE_ROWS * PASSES, :].bitcast(I32),
+                in_=scales_dram[m].bitcast(I32)[:, SCALE_ROWS * quadrant : SCALE_ROWS * (quadrant + 1), :],
+            )
+
+    def load_rows(m):
         rows = acts.tile([P, BATCH_TILES, DEPTH], BF16, name="rows%d" % m)
         a_rows.append(rows)
-        tiles = BATCH_TILES // ROW_LOADS
-        for i in range(ROW_LOADS):
+        tiles = BATCH_TILES // ROW_LOADS[m]
+        for i in range(ROW_LOADS[m]):
             nc.sync.dma_start(
                 out=rows[:, tiles * i : tiles * (i + 1), :],
                 in_=rows_dram[m][tiles * P * i : tiles * P * (i + 1), :].rearrange("(t b) k -> b t k", b=P),
             )
 
-    scales_dram = (kernel_scales, recurrent_kernel_scales)
-    for quadrant in range(4):
-        for m in (FROM_X, FROM_H):
-            first = 32 * quadrant + 4 * PASSES * m
-            nc.sync.dma_start(
-                out=w_planes[first : first + 4 * PASSES, :].bitcast(I32),
-                in_=scales_dram[m].bitcast(I32)[:, 4 * quadrant : 4 * quadrant + 4, :],
-            )
+    def load_words(m, gate, bank):
+        words = weights.tile([P, PASSES, BANK], U32, name="w%d_%d_%d" % (m, gate, bank), align_bytes=64)
+        w_words[(m, gate, bank)] = words
+        first = gate * UNITS + bank * BANK
+        nc.sync.dma_start(
+            out=words[:].bitcast(I32),
+            in_=words_dram[m]
+            .rearrange("g p n t -> g p (n t)")
+            .bitcast(I32)[:, :, first : first + BANK]
+            .rearrange("g p n -> p g n"),
+        )
 
-    words_dram = (kernel_words, recurrent_kernel_words)
-    w_words = {}
-    for load in range(UNIT_TILES // LOAD_TILES):
-        for m, gate in ((FROM_X, GATE_H), (FROM_X, GATE_R), (FROM_H, GATE_R), (FROM_H, GATE_H), (FROM_X, GATE_Z), (FROM_H, GATE_Z)):
-            words = weights.tile([P, PASSES, LOAD_COLS], U32, name="w%d_%d_%d" % (m, gate, load), align_bytes=64)
-            w_words[(m, gate, load)] = words
-            first = gate * UNITS + load * LOAD_COLS
-            nc.sync.dma_start(
-                out=words[:].bitcast(I32),
-                in_=words_dram[m]
-                .rearrange("g p n t -> g p (n t)")
-                .bitcast(I32)[:, :, first : first + LOAD_COLS]
-                .rearrange("g p n -> p g n"),
-            )
+    load_rows(FROM_X)
+    load_scales(FROM_X)
+    load_rows(FROM_H)
+    load_scales(FROM_H)
+    for bank in range(BANKS_PER_GATE):
+        load_words(FROM_X, GATE_Z, bank)
+        load_words(FROM_H, GATE_Z, bank)
+    for bank in range(BANKS_PER_GATE):
+        load_words(FROM_X, GATE_R, bank)
+        load_words(FROM_H, GATE_R, bank)
+        load_words(FROM_H, GATE_H, bank)
+        load_words(FROM_X, GATE_H, bank)
 
     a_codes = []
     a_scales = []
     with tc.psum_pool(name="prep_psum", bufs=1) as prep_psum:
-
-        def transpose_and_quantise(m):
+        for m in (FROM_X, FROM_H):
             grouped = acts.tile([P, PASSES, BATCH, PACK], BF16, name="grouped%d" % m, align_bytes=64)
             grouped_words = (
                 grouped[:]
@@ -126,9 +131,14 @@ def gru_cell(
                 .bitcast(F32)
                 .rearrange("p (g c u) -> p g c u", g=PASSES, u=HALVES)
             )
+            codes = acts.tile([P, PASSES, BATCH], U32, name="codes%d" % m, align_bytes=64)
+            scales = acts.tile([P, PASSES, BATCH], U8, name="scales%d" % m, align_bytes=64)
+            a_codes.append(codes)
+            a_scales.append(scales)
             for t in range(BATCH_TILES):
+                cols = slice(t * P, (t + 1) * P)
                 row_words = a_rows[m][:, t, :].bitcast(F32)
-                flipped = prep_psum.tile([P, PASSES, HALVES, P], F32, tag="flipped", bufs=4)
+                flipped = prep_psum.tile([P, PASSES, HALVES, P], F32, bufs=4)
                 for g in range(PASSES):
                     for u in range(HALVES):
                         nc.tensor.transpose(
@@ -136,20 +146,13 @@ def gru_cell(
                             row_words[:, F32_PER_PASS * g + u : F32_PER_PASS * (g + 1) : HALVES],
                             ident_f32[:],
                         )
-                copy = nc.vector.tensor_copy if t % 2 == 0 else nc.scalar.copy
-                copy(out=grouped_words[:, :, t * P : (t + 1) * P, :], in_=flipped[:].rearrange("p g u b -> p g b u"))
-            codes = acts.tile([P, PASSES, BATCH], U32, name="codes%d" % m, align_bytes=64)
-            scales = acts.tile([P, PASSES, BATCH], U8, name="scales%d" % m, align_bytes=64)
-            for g in range(PASSES):
-                nc.vector.quantize_mx(
-                    out=codes[:, g, :].bitcast(FP8X4),
-                    scales=scales[:, g, :],
-                    in_=grouped[:, g, :, :].rearrange("p c t -> p (c t)"),
-                )
-            a_codes.append(codes)
-            a_scales.append(scales)
-
-        transpose_and_quantise(FROM_X)
+                nc.scalar.copy(out=grouped_words[:, :, cols, :], in_=flipped[:].rearrange("p g u b -> p g b u"))
+                for g in range(PASSES):
+                    nc.vector.quantize_mx(
+                        out=codes[:, g, cols].bitcast(FP8X4),
+                        scales=scales[:, g, cols],
+                        in_=grouped[:, g, cols, :].rearrange("p c t -> p (c t)"),
+                    )
 
         bias_cols_ps = prep_psum.tile([P, P], BF16)
         nc.tensor.transpose(bias_cols_ps[:], bias_rows[:], ident_bf16[:])
@@ -161,111 +164,112 @@ def gru_cell(
         nc.vector.tensor_tensor(out=r_bias[:], in0=bias_cols[:, 0, GATE_R, :], in1=bias_cols[:, 1, GATE_R, :], op=ALU.add)
         nc.vector.tensor_scalar(out=r_bias[:], in0=r_bias[:], scalar1=0.2, scalar2=0.5, op0=ALU.mult, op1=ALU.add)
         z_bias = consts.tile([P, UNITS], F32)
-        for c in range(UNITS // BANK):
+        for bank in range(BANKS_PER_GATE):
             z_bias_ps = prep_psum.tile([P, BANK], F32, bufs=2)
-            nc.tensor.matmul(z_bias_ps[:], lhsT=ones[:], rhs=z_bias_rows[:, c * BANK : (c + 1) * BANK], start=True, stop=True)
+            nc.tensor.matmul(z_bias_ps[:], lhsT=ones[:], rhs=z_bias_rows[:, bank * BANK : (bank + 1) * BANK], start=True, stop=True)
             nc.vector.tensor_scalar(
-                out=z_bias[:, c * BANK : (c + 1) * BANK], in0=z_bias_ps[:], scalar1=0.2, scalar2=0.5, op0=ALU.mult, op1=ALU.add
+                out=z_bias[:, bank * BANK : (bank + 1) * BANK], in0=z_bias_ps[:], scalar1=0.2, scalar2=0.5, op0=ALU.mult, op1=ALU.add
             )
 
-        transpose_and_quantise(FROM_H)
+    def weight_plane(m, g, first_col, cols):
+        return w_planes[SCALE_ROWS * (PASSES * m + g) : P, first_col : first_col + cols]
 
-    psum = ctx.enter_context(tc.psum_pool(name="psum", bufs=1, reuse_waits="tile"))
+    both = [(m, g) for m in (FROM_X, FROM_H) for g in range(PASSES)]
 
-    def weight_operand(m, gate, j, g):
-        load, inside = divmod(j, LOAD_TILES)
-        first_row = 4 * (PASSES * m + g)
-        first_col = gate * UNITS + j * P
-        return (
-            w_words[(m, gate, load)][:, g, inside * P : (inside + 1) * P].bitcast(FP8X4),
-            w_planes[first_row:P, first_col : first_col + P],
-        )
-
-    def units_by_batch(acc, gate, j, sources):
-        passes = [(m, g) for m in sources for g in range(PASSES)]
-        for i, (m, g) in enumerate(passes):
-            words, plane = weight_operand(m, gate, j, g)
-            nc.tensor.matmul_mx(
-                out=acc,
-                lhsT=words,
-                lhsT_scale=plane,
-                rhs=a_codes[m][:, g, :].bitcast(FP8X4),
-                rhs_scale=a_scales[m][:, g, :],
-                start=(i == 0),
-                stop=(i == len(passes) - 1),
-            )
-
-    def batch_by_units(acc, gate, j, sources):
-        passes = [(m, g) for m in sources for g in range(PASSES)]
-        for t in range(BATCH_TILES):
-            for i, (m, g) in enumerate(passes):
-                words, plane = weight_operand(m, gate, j, g)
-                nc.tensor.matmul_mx(
-                    out=acc[:, t, :],
-                    lhsT=a_codes[m][:, g, t * P : (t + 1) * P].bitcast(FP8X4),
-                    lhsT_scale=a_scales[m][:, g, t * P : (t + 1) * P],
-                    rhs=words,
-                    rhs_scale=plane,
-                    start=(i == 0),
-                    stop=(i == len(passes) - 1),
+    z_h = acts.tile([P, BATCH_TILES, UNITS], F32)
+    not_z = acts.tile([P, BATCH_TILES, UNITS], F32)
+    blocks = [(bank, t) for bank in range(BANKS_PER_GATE) for t in range(BATCH_TILES)]
+    z_relu = {}
+    with tc.psum_pool(name="z_psum", bufs=4, reuse_waits="tile") as z_psum:
+        for i in range(len(blocks) + Z_LAG):
+            if i < len(blocks):
+                bank, t = blocks[i]
+                units = slice(bank * BANK, (bank + 1) * BANK)
+                acc_z = z_psum.tile([P, BANK], F32)
+                for m, g in both:
+                    nc.tensor.matmul_mx(
+                        out=acc_z[:],
+                        lhsT=a_codes[m][:, g, t * P : (t + 1) * P].bitcast(FP8X4),
+                        lhsT_scale=a_scales[m][:, g, t * P : (t + 1) * P],
+                        rhs=w_words[(m, GATE_Z, bank)][:, g, :].bitcast(FP8X4),
+                        rhs_scale=weight_plane(m, g, GATE_Z * UNITS + bank * BANK, BANK),
+                        start=((m, g) == both[0]),
+                        stop=((m, g) == both[-1]),
+                    )
+                z_line = work.tile([P, BANK], F32)
+                nc.vector.scalar_tensor_tensor(
+                    out=z_line[:], in0=acc_z[:], scalar=0.2, in1=z_bias[:, units], op0=ALU.mult, op1=ALU.add
+                )
+                z_relu[i] = work.tile([P, BANK], F32, name="z_relu", bufs=Z_LAG + 1)
+                nc.scalar.activation(out=z_relu[i][:], in_=z_line[:], func=ACT.Relu)
+                nc.scalar.activation(out=not_z[:, t, units], in_=z_line[:], func=ACT.Relu, bias=1.0, scale=-1.0)
+            if i >= Z_LAG:
+                bank, t = blocks[i - Z_LAG]
+                units = slice(bank * BANK, (bank + 1) * BANK)
+                nc.vector.scalar_tensor_tensor(
+                    out=z_h[:, t, units],
+                    in0=z_relu[i - Z_LAG][:],
+                    scalar=1.0,
+                    in1=a_rows[FROM_H][:, t, units],
+                    op0=ALU.min,
+                    op1=ALU.mult,
                 )
 
+    psum = ctx.enter_context(tc.psum_pool(name="psum", bufs=2, reuse_waits="tile"))
     out_tiles = out.rearrange("(t b) n -> b t n", b=P)
 
-    def to_batch_by_units(cand):
-        cand_t = psum.tile([P, BATCH_TILES, P], F32, bufs=2)
-        for t in range(BATCH_TILES):
-            nc.tensor.transpose(cand_t[:, t, :], cand[:, t * P : (t + 1) * P], ident_f32[:])
-        return cand_t
+    def units_by_batch(acc, gate, j, passes):
+        bank, inside = divmod(j, TILES_PER_BANK)
+        for m, g in passes:
+            nc.tensor.matmul_mx(
+                out=acc,
+                lhsT=w_words[(m, gate, bank)][:, g, inside * P : (inside + 1) * P].bitcast(FP8X4),
+                lhsT_scale=weight_plane(m, g, gate * UNITS + j * P, P),
+                rhs=a_codes[m][:, g, :].bitcast(FP8X4),
+                rhs_scale=a_scales[m][:, g, :],
+                start=((m, g) == passes[0]),
+                stop=((m, g) == passes[-1]),
+            )
 
-    def blend(j, cand_t, z_relu):
-        units = slice(j * P, (j + 1) * P)
-        diff = work.tile([P, BATCH_TILES, P], F32)
-        nc.vector.tensor_tensor(out=diff[:], in0=a_rows[FROM_H][:, :, units], in1=cand_t[:], op=ALU.subtract)
-        z_diff = work.tile([P, BATCH_TILES, P], F32)
-        nc.vector.scalar_tensor_tensor(out=z_diff[:], in0=z_relu[:], scalar=1.0, in1=diff[:], op0=ALU.min, op1=ALU.mult)
-        result = work.tile([P, BATCH_TILES, P], F32)
-        nc.vector.tensor_tensor(out=result[:], in0=z_diff[:], in1=cand_t[:], op=ALU.add)
-        nc.sync.dma_start(out=out_tiles[:, :, units], in_=result[:])
+    pre_tanh = {}
+    cand = {}
+    for j in range(UNIT_TILES + 2):
+        if j < UNIT_TILES:
+            acc_r = psum.tile([P, BATCH], F32)
+            units_by_batch(acc_r[:], GATE_R, j, both)
+            acc_rh = psum.tile([P, BATCH], F32)
+            units_by_batch(acc_rh[:], GATE_H, j, both[PASSES:])
+            acc_xh = psum.tile([P, BATCH], F32)
+            units_by_batch(acc_xh[:], GATE_H, j, both[:PASSES])
+        if j >= 2:
+            cand_t = psum.tile([P, BATCH_TILES, P], F32)
+            for t in range(BATCH_TILES):
+                nc.tensor.transpose(cand_t[:, t, :], cand[j - 2][:, t * P : (t + 1) * P], ident_f32[:])
 
-    cand = None
-    z_relu = None
-    for j in range(UNIT_TILES):
-        acc_xh = psum.tile([P, BATCH], F32, bufs=2)
-        units_by_batch(acc_xh[:], GATE_H, j, (FROM_X,))
-        acc_r = psum.tile([P, BATCH], F32)
-        units_by_batch(acc_r[:], GATE_R, j, (FROM_X, FROM_H))
-        acc_rh = psum.tile([P, BATCH], F32)
-        units_by_batch(acc_rh[:], GATE_H, j, (FROM_H,))
-        acc_z = psum.tile([P, BATCH_TILES, P], F32, bufs=2)
-        batch_by_units(acc_z, GATE_Z, j, (FROM_X, FROM_H))
-        if j > 0:
-            cand_t = to_batch_by_units(cand)
-            z_before = z_relu
+        if j < UNIT_TILES:
+            r_relu = work.tile([P, BATCH], F32)
+            nc.scalar.activation(out=r_relu[:], in_=acc_r[:], func=ACT.Relu, bias=r_bias[:, j : j + 1], scale=0.2)
+            rec_h = work.tile([P, BATCH], F32)
+            nc.scalar.activation(out=rec_h[:], in_=acc_rh[:], func=ACT.Identity, bias=bias_cols[:, 1, GATE_H, j : j + 1], scale=1.0)
+        if 1 <= j <= UNIT_TILES:
+            cand[j - 1] = work.tile([P, BATCH], F32, name="cand", bufs=3)
+            nc.scalar.activation(
+                out=cand[j - 1][:], in_=pre_tanh[j - 1][:], func=ACT.Tanh, bias=bias_cols[:, 0, GATE_H, j - 1 : j], scale=1.0
+            )
 
-        r_relu = work.tile([P, BATCH], F32)
-        nc.scalar.activation(out=r_relu[:], in_=acc_r[:], func=ACT.Relu, bias=r_bias[:, j : j + 1], scale=0.2)
-        rec_h = work.tile([P, BATCH], F32)
-        nc.scalar.activation(out=rec_h[:], in_=acc_rh[:], func=ACT.Identity, bias=bias_cols[:, 1, GATE_H, j : j + 1], scale=1.0)
-        gated = work.tile([P, BATCH], F32)
-        nc.vector.scalar_tensor_tensor(out=gated[:], in0=r_relu[:], scalar=1.0, in1=rec_h[:], op0=ALU.min, op1=ALU.mult)
-        pre_tanh = work.tile([P, BATCH], F32)
-        nc.vector.tensor_tensor(out=pre_tanh[:], in0=acc_xh[:], in1=gated[:], op=ALU.add)
-        cand = work.tile([P, BATCH], F32)
-        nc.scalar.activation(out=cand[:], in_=pre_tanh[:], func=ACT.Tanh, bias=bias_cols[:, 0, GATE_H, j : j + 1], scale=1.0)
-
-        z_line = work.tile([P, BATCH_TILES, P], F32)
-        nc.vector.scalar_tensor_tensor(
-            out=z_line[:],
-            in0=acc_z[:],
-            scalar=0.2,
-            in1=z_bias[:, j * P : (j + 1) * P].unsqueeze(1).to_broadcast([P, BATCH_TILES, P]),
-            op0=ALU.mult,
-            op1=ALU.add,
-        )
-        z_relu = work.tile([P, BATCH_TILES, P], F32)
-        nc.scalar.activation(out=z_relu[:], in_=z_line[:], func=ACT.Relu)
-
-        if j > 0:
-            blend(j - 1, cand_t, z_before)
-    blend(UNIT_TILES - 1, to_batch_by_units(cand), z_relu)
+        units = slice((j - 2) * P, (j - 1) * P)
+        if j < UNIT_TILES:
+            gated = work.tile([P, BATCH], F32)
+            nc.vector.scalar_tensor_tensor(out=gated[:], in0=r_relu[:], scalar=1.0, in1=rec_h[:], op0=ALU.min, op1=ALU.mult)
+        if j >= 2:
+            fresh = work.tile([P, BATCH_TILES, P], F32)
+            nc.vector.scalar_tensor_tensor(
+                out=fresh[:], in0=not_z[:, :, units], scalar=1.0, in1=cand_t[:], op0=ALU.min, op1=ALU.mult
+            )
+        if j < UNIT_TILES:
+            pre_tanh[j] = work.tile([P, BATCH], F32, name="pre_tanh")
+            nc.vector.tensor_tensor(out=pre_tanh[j][:], in0=acc_xh[:], in1=gated[:], op=ALU.add)
+        if j >= 2:
+            result = work.tile([P, BATCH_TILES, P], F32, bufs=3)
+            nc.vector.tensor_tensor(out=result[:], in0=fresh[:], in1=z_h[:, :, units], op=ALU.add)
+            nc.sync.dma_start(out=out_tiles[:, :, units], in_=result[:])

@@ -31,6 +31,7 @@ TILES_PER_BANK = BANK // P
 SCALE_ROWS = 4
 ROW_LOADS = (2, 4)
 Z_LAG = 2
+TAIL_TILES = 2
 
 FLOPS = 2 * 2 * BATCH * DEPTH * 3 * UNITS
 
@@ -77,12 +78,13 @@ def gru_cell(
     a_rows = []
     w_words = {}
 
-    def load_scales(m):
+    def load_scales(m, first_gate, gates):
+        cols = slice(first_gate * UNITS, (first_gate + gates) * UNITS)
         for quadrant in range(4):
             first = 32 * quadrant + SCALE_ROWS * PASSES * m
             nc.sync.dma_start(
-                out=w_planes[first : first + SCALE_ROWS * PASSES, :].bitcast(I32),
-                in_=scales_dram[m].bitcast(I32)[:, SCALE_ROWS * quadrant : SCALE_ROWS * (quadrant + 1), :],
+                out=w_planes[first : first + SCALE_ROWS * PASSES, cols].bitcast(I32),
+                in_=scales_dram[m][:, SCALE_ROWS * quadrant : SCALE_ROWS * (quadrant + 1), cols].bitcast(I32),
             )
 
     def load_rows(m):
@@ -108,12 +110,14 @@ def gru_cell(
         )
 
     load_rows(FROM_X)
-    load_scales(FROM_X)
+    load_scales(FROM_X, GATE_Z, 1)
     load_rows(FROM_H)
-    load_scales(FROM_H)
+    load_scales(FROM_H, GATE_Z, 1)
     for bank in range(BANKS_PER_GATE):
         load_words(FROM_X, GATE_Z, bank)
         load_words(FROM_H, GATE_Z, bank)
+    load_scales(FROM_X, GATE_R, 2)
+    load_scales(FROM_H, GATE_R, 2)
     for bank in range(BANKS_PER_GATE):
         load_words(FROM_X, GATE_R, bank)
         load_words(FROM_H, GATE_R, bank)
@@ -179,36 +183,44 @@ def gru_cell(
     z_h = acts.tile([P, BATCH_TILES, UNITS], F32)
     not_z = acts.tile([P, BATCH_TILES, UNITS], F32)
     blocks = [(bank, t) for bank in range(BANKS_PER_GATE) for t in range(BATCH_TILES)]
+    acc_z = {}
     z_relu = {}
     with tc.psum_pool(name="z_psum", bufs=4, reuse_waits="tile") as z_psum:
-        for i in range(len(blocks) + Z_LAG):
+
+        def z_passes(i, m):
+            bank, t = blocks[i]
+            for g in range(PASSES):
+                nc.tensor.matmul_mx(
+                    out=acc_z[i][:],
+                    lhsT=a_codes[m][:, g, t * P : (t + 1) * P].bitcast(FP8X4),
+                    lhsT_scale=a_scales[m][:, g, t * P : (t + 1) * P],
+                    rhs=w_words[(m, GATE_Z, bank)][:, g, :].bitcast(FP8X4),
+                    rhs_scale=weight_plane(m, g, GATE_Z * UNITS + bank * BANK, BANK),
+                    start=((m, g) == both[0]),
+                    stop=((m, g) == both[-1]),
+                )
+
+        for i in range(len(blocks) + 1 + Z_LAG):
             if i < len(blocks):
-                bank, t = blocks[i]
+                acc_z[i] = z_psum.tile([P, BANK], F32, name="acc_z")
+                z_passes(i, FROM_X)
+            if 1 <= i <= len(blocks):
+                bank, t = blocks[i - 1]
                 units = slice(bank * BANK, (bank + 1) * BANK)
-                acc_z = z_psum.tile([P, BANK], F32)
-                for m, g in both:
-                    nc.tensor.matmul_mx(
-                        out=acc_z[:],
-                        lhsT=a_codes[m][:, g, t * P : (t + 1) * P].bitcast(FP8X4),
-                        lhsT_scale=a_scales[m][:, g, t * P : (t + 1) * P],
-                        rhs=w_words[(m, GATE_Z, bank)][:, g, :].bitcast(FP8X4),
-                        rhs_scale=weight_plane(m, g, GATE_Z * UNITS + bank * BANK, BANK),
-                        start=((m, g) == both[0]),
-                        stop=((m, g) == both[-1]),
-                    )
+                z_passes(i - 1, FROM_H)
                 z_line = work.tile([P, BANK], F32)
                 nc.vector.scalar_tensor_tensor(
-                    out=z_line[:], in0=acc_z[:], scalar=0.2, in1=z_bias[:, units], op0=ALU.mult, op1=ALU.add
+                    out=z_line[:], in0=acc_z[i - 1][:], scalar=0.2, in1=z_bias[:, units], op0=ALU.mult, op1=ALU.add
                 )
-                z_relu[i] = work.tile([P, BANK], F32, name="z_relu", bufs=Z_LAG + 1)
-                nc.scalar.activation(out=z_relu[i][:], in_=z_line[:], func=ACT.Relu)
+                z_relu[i - 1] = work.tile([P, BANK], F32, name="z_relu", bufs=Z_LAG + 1)
+                nc.scalar.activation(out=z_relu[i - 1][:], in_=z_line[:], func=ACT.Relu)
                 nc.scalar.activation(out=not_z[:, t, units], in_=z_line[:], func=ACT.Relu, bias=1.0, scale=-1.0)
-            if i >= Z_LAG:
-                bank, t = blocks[i - Z_LAG]
+            if i > Z_LAG:
+                bank, t = blocks[i - 1 - Z_LAG]
                 units = slice(bank * BANK, (bank + 1) * BANK)
                 nc.vector.scalar_tensor_tensor(
                     out=z_h[:, t, units],
-                    in0=z_relu[i - Z_LAG][:],
+                    in0=z_relu[i - 1 - Z_LAG][:],
                     scalar=1.0,
                     in1=a_rows[FROM_H][:, t, units],
                     op0=ALU.min,
@@ -218,58 +230,76 @@ def gru_cell(
     psum = ctx.enter_context(tc.psum_pool(name="psum", bufs=2, reuse_waits="tile"))
     out_tiles = out.rearrange("(t b) n -> b t n", b=P)
 
-    def units_by_batch(acc, gate, j, passes):
+    def units_by_batch(acc, gate, j, batch, passes):
         bank, inside = divmod(j, TILES_PER_BANK)
         for m, g in passes:
             nc.tensor.matmul_mx(
                 out=acc,
                 lhsT=w_words[(m, gate, bank)][:, g, inside * P : (inside + 1) * P].bitcast(FP8X4),
                 lhsT_scale=weight_plane(m, g, gate * UNITS + j * P, P),
-                rhs=a_codes[m][:, g, :].bitcast(FP8X4),
-                rhs_scale=a_scales[m][:, g, :],
+                rhs=a_codes[m][:, g, batch].bitcast(FP8X4),
+                rhs_scale=a_scales[m][:, g, batch],
                 start=((m, g) == passes[0]),
                 stop=((m, g) == passes[-1]),
             )
 
+    pieces = [(j, 0, BATCH_TILES) for j in range(UNIT_TILES - 1)]
+    pieces.extend([(UNIT_TILES - 1, first, TAIL_TILES) for first in range(0, BATCH_TILES, TAIL_TILES)])
+
     pre_tanh = {}
     cand = {}
-    for j in range(UNIT_TILES + 2):
-        if j < UNIT_TILES:
+    for k in range(len(pieces) + 2):
+        if k < len(pieces):
+            j, first, count = pieces[k]
+            batch = slice(first * P, (first + count) * P)
+            width = count * P
             acc_r = psum.tile([P, BATCH], F32)
-            units_by_batch(acc_r[:], GATE_R, j, both)
+            units_by_batch(acc_r[:, :width], GATE_R, j, batch, both)
             acc_rh = psum.tile([P, BATCH], F32)
-            units_by_batch(acc_rh[:], GATE_H, j, both[PASSES:])
+            units_by_batch(acc_rh[:, :width], GATE_H, j, batch, both[PASSES:])
             acc_xh = psum.tile([P, BATCH], F32)
-            units_by_batch(acc_xh[:], GATE_H, j, both[:PASSES])
-        if j >= 2:
+            units_by_batch(acc_xh[:, :width], GATE_H, j, batch, both[:PASSES])
+        if k >= 2:
+            end_j, end_first, end_count = pieces[k - 2]
             cand_t = psum.tile([P, BATCH_TILES, P], F32)
-            for t in range(BATCH_TILES):
-                nc.tensor.transpose(cand_t[:, t, :], cand[j - 2][:, t * P : (t + 1) * P], ident_f32[:])
+            for t in range(end_count):
+                nc.tensor.transpose(cand_t[:, t, :], cand[k - 2][:, t * P : (t + 1) * P], ident_f32[:])
 
-        if j < UNIT_TILES:
+        if k < len(pieces):
             r_relu = work.tile([P, BATCH], F32)
-            nc.scalar.activation(out=r_relu[:], in_=acc_r[:], func=ACT.Relu, bias=r_bias[:, j : j + 1], scale=0.2)
+            nc.scalar.activation(out=r_relu[:, :width], in_=acc_r[:, :width], func=ACT.Relu, bias=r_bias[:, j : j + 1], scale=0.2)
             rec_h = work.tile([P, BATCH], F32)
-            nc.scalar.activation(out=rec_h[:], in_=acc_rh[:], func=ACT.Identity, bias=bias_cols[:, 1, GATE_H, j : j + 1], scale=1.0)
-        if 1 <= j <= UNIT_TILES:
-            cand[j - 1] = work.tile([P, BATCH], F32, name="cand", bufs=3)
             nc.scalar.activation(
-                out=cand[j - 1][:], in_=pre_tanh[j - 1][:], func=ACT.Tanh, bias=bias_cols[:, 0, GATE_H, j - 1 : j], scale=1.0
+                out=rec_h[:, :width], in_=acc_rh[:, :width], func=ACT.Identity, bias=bias_cols[:, 1, GATE_H, j : j + 1], scale=1.0
+            )
+        if 1 <= k <= len(pieces):
+            tanh_j, tanh_first, tanh_count = pieces[k - 1]
+            tanh_width = tanh_count * P
+            cand[k - 1] = work.tile([P, BATCH], F32, name="cand", bufs=3)
+            nc.scalar.activation(
+                out=cand[k - 1][:, :tanh_width],
+                in_=pre_tanh[k - 1][:, :tanh_width],
+                func=ACT.Tanh,
+                bias=bias_cols[:, 0, GATE_H, tanh_j : tanh_j + 1],
+                scale=1.0,
             )
 
-        units = slice((j - 2) * P, (j - 1) * P)
-        if j < UNIT_TILES:
+        if k < len(pieces):
             gated = work.tile([P, BATCH], F32)
-            nc.vector.scalar_tensor_tensor(out=gated[:], in0=r_relu[:], scalar=1.0, in1=rec_h[:], op0=ALU.min, op1=ALU.mult)
-        if j >= 2:
+            nc.vector.scalar_tensor_tensor(
+                out=gated[:, :width], in0=r_relu[:, :width], scalar=1.0, in1=rec_h[:, :width], op0=ALU.min, op1=ALU.mult
+            )
+        if k >= 2:
+            units = slice(end_j * P, (end_j + 1) * P)
+            tiles = slice(end_first, end_first + end_count)
             fresh = work.tile([P, BATCH_TILES, P], F32)
             nc.vector.scalar_tensor_tensor(
-                out=fresh[:], in0=not_z[:, :, units], scalar=1.0, in1=cand_t[:], op0=ALU.min, op1=ALU.mult
+                out=fresh[:, :end_count, :], in0=not_z[:, tiles, units], scalar=1.0, in1=cand_t[:, :end_count, :], op0=ALU.min, op1=ALU.mult
             )
-        if j < UNIT_TILES:
-            pre_tanh[j] = work.tile([P, BATCH], F32, name="pre_tanh")
-            nc.vector.tensor_tensor(out=pre_tanh[j][:], in0=acc_xh[:], in1=gated[:], op=ALU.add)
-        if j >= 2:
+        if k < len(pieces):
+            pre_tanh[k] = work.tile([P, BATCH], F32, name="pre_tanh")
+            nc.vector.tensor_tensor(out=pre_tanh[k][:, :width], in0=acc_xh[:, :width], in1=gated[:, :width], op=ALU.add)
+        if k >= 2:
             result = work.tile([P, BATCH_TILES, P], F32, bufs=3)
-            nc.vector.tensor_tensor(out=result[:], in0=fresh[:], in1=z_h[:, :, units], op=ALU.add)
-            nc.sync.dma_start(out=out_tiles[:, :, units], in_=result[:])
+            nc.vector.tensor_tensor(out=result[:, :end_count, :], in0=fresh[:, :end_count, :], in1=z_h[:, tiles, units], op=ALU.add)
+            nc.sync.dma_start(out=out_tiles[:, tiles, units], in_=result[:, :end_count, :])

@@ -29,7 +29,8 @@ BANK = 512
 BANKS_PER_GATE = UNITS // BANK
 TILES_PER_BANK = BANK // P
 SCALE_ROWS = 4
-ROW_LOADS = (2, 4)
+VECTOR_COPIES = ((FROM_H, 1),)
+X_LEAD = 2
 Z_LAG = 2
 TAIL_TILES = 2
 
@@ -55,27 +56,31 @@ def gru_cell(
     weights = ctx.enter_context(tc.tile_pool(name="weights", bufs=1))
     work = ctx.enter_context(tc.tile_pool(name="work", bufs=2))
 
+    ones = consts.tile([P, P], BF16)
+    nc.vector.memset(ones[:], 1.0)
     w_planes = consts.tile([P, 3 * UNITS], U8, align_bytes=64)
-    nc.vector.memset(w_planes[:].bitcast(I32), 0)
+    nc.vector.memset(w_planes[:, GATE_Z * UNITS : (GATE_Z + 1) * UNITS].bitcast(I32), 0)
+
+    bias_rows = consts.tile([P, P], BF16)
+    nc.vector.memset(bias_rows[:].bitcast(I32), 0)
+    z_bias_rows = consts.tile([P, UNITS], BF16)
+    nc.vector.memset(z_bias_rows[:].bitcast(I32), 0)
+    unread = consts.tile([P, 1], F32)
+    nc.scalar.activation(out=unread[:], in_=ones[:, 0:1], func=ACT.Tanh)
+
+    nc.vector.memset(w_planes[:, GATE_R * UNITS : (GATE_H + 1) * UNITS].bitcast(I32), 0)
 
     ident_f32 = consts.tile([P, P], F32)
     make_identity(nc, ident_f32[:])
-
-    bias_rows = consts.tile([P, P], BF16)
-    nc.vector.memset(bias_rows[:], 0.0)
-    nc.scalar.dma_start(out=bias_rows[0 : 2 * 3 * UNIT_TILES, :], in_=bias.rearrange("b (c n) -> (b c) n", n=P))
-    z_bias_rows = consts.tile([P, UNITS], BF16)
-    nc.vector.memset(z_bias_rows[:], 0.0)
-    nc.scalar.dma_start(out=z_bias_rows[0:2, :], in_=bias[:, GATE_Z * UNITS : (GATE_Z + 1) * UNITS])
-    ones = consts.tile([P, P], BF16)
-    nc.vector.memset(ones[:], 1.0)
+    nc.gpsimd.dma_start(out=z_bias_rows[0:2, :], in_=bias[:, GATE_Z * UNITS : (GATE_Z + 1) * UNITS])
+    nc.gpsimd.dma_start(out=bias_rows[0 : 2 * 3 * UNIT_TILES, :], in_=bias.rearrange("b (c n) -> (b c) n", n=P))
     ident_bf16 = consts.tile([P, P], BF16)
     make_identity(nc, ident_bf16[:])
 
     rows_dram = (inputs, h_tm1)
     scales_dram = (kernel_scales, recurrent_kernel_scales)
     words_dram = (kernel_words, recurrent_kernel_words)
-    a_rows = []
+    a_rows = [acts.tile([P, BATCH_TILES, DEPTH], BF16, name="rows%d" % m) for m in (FROM_X, FROM_H)]
     w_words = {}
 
     def load_scales(m, first_gate, gates):
@@ -87,15 +92,11 @@ def gru_cell(
                 in_=scales_dram[m][:, SCALE_ROWS * quadrant : SCALE_ROWS * (quadrant + 1), cols].bitcast(I32),
             )
 
-    def load_rows(m):
-        rows = acts.tile([P, BATCH_TILES, DEPTH], BF16, name="rows%d" % m)
-        a_rows.append(rows)
-        tiles = BATCH_TILES // ROW_LOADS[m]
-        for i in range(ROW_LOADS[m]):
-            nc.sync.dma_start(
-                out=rows[:, tiles * i : tiles * (i + 1), :],
-                in_=rows_dram[m][tiles * P * i : tiles * P * (i + 1), :].rearrange("(t b) k -> b t k", b=P),
-            )
+    def load_rows(m, first, tiles):
+        nc.sync.dma_start(
+            out=a_rows[m][:, first : first + tiles, :],
+            in_=rows_dram[m][P * first : P * (first + tiles), :].rearrange("(t b) k -> b t k", b=P),
+        )
 
     def load_words(m, gate, bank):
         words = weights.tile([P, PASSES, BANK], U32, name="w%d_%d_%d" % (m, gate, bank), align_bytes=64)
@@ -109,13 +110,17 @@ def gru_cell(
             .rearrange("g p n -> p g n"),
         )
 
-    load_rows(FROM_X)
+    load_rows(FROM_X, 0, 1)
+    load_rows(FROM_X, 1, 1)
+    load_rows(FROM_X, 2, 2)
+    load_rows(FROM_H, 0, 2)
     load_scales(FROM_X, GATE_Z, 1)
-    load_rows(FROM_H)
+    load_rows(FROM_H, 2, 2)
+    load_words(FROM_X, GATE_Z, 0)
     load_scales(FROM_H, GATE_Z, 1)
-    for bank in range(BANKS_PER_GATE):
-        load_words(FROM_X, GATE_Z, bank)
-        load_words(FROM_H, GATE_Z, bank)
+    load_words(FROM_H, GATE_Z, 0)
+    load_words(FROM_X, GATE_Z, 1)
+    load_words(FROM_H, GATE_Z, 1)
     load_scales(FROM_X, GATE_R, 2)
     load_scales(FROM_H, GATE_R, 2)
     for bank in range(BANKS_PER_GATE):
@@ -124,56 +129,78 @@ def gru_cell(
         load_words(FROM_H, GATE_H, bank)
         load_words(FROM_X, GATE_H, bank)
 
+    psum = ctx.enter_context(tc.psum_pool(name="psum", bufs=8))
+
+    grouped = {}
     a_codes = []
     a_scales = []
-    with tc.psum_pool(name="prep_psum", bufs=1) as prep_psum:
-        for m in (FROM_X, FROM_H):
-            grouped = acts.tile([P, PASSES, BATCH, PACK], BF16, name="grouped%d" % m, align_bytes=64)
-            grouped_words = (
-                grouped[:]
-                .rearrange("p g c t -> p (g c t)")
-                .bitcast(F32)
-                .rearrange("p (g c u) -> p g c u", g=PASSES, u=HALVES)
-            )
-            codes = acts.tile([P, PASSES, BATCH], U32, name="codes%d" % m, align_bytes=64)
-            scales = acts.tile([P, PASSES, BATCH], U8, name="scales%d" % m, align_bytes=64)
-            a_codes.append(codes)
-            a_scales.append(scales)
-            for t in range(BATCH_TILES):
-                cols = slice(t * P, (t + 1) * P)
-                row_words = a_rows[m][:, t, :].bitcast(F32)
-                flipped = prep_psum.tile([P, PASSES, HALVES, P], F32, bufs=4)
-                for g in range(PASSES):
-                    for u in range(HALVES):
-                        nc.tensor.transpose(
-                            flipped[:, g, u, :],
-                            row_words[:, F32_PER_PASS * g + u : F32_PER_PASS * (g + 1) : HALVES],
-                            ident_f32[:],
-                        )
-                nc.scalar.copy(out=grouped_words[:, :, cols, :], in_=flipped[:].rearrange("p g u b -> p g b u"))
-                for g in range(PASSES):
-                    nc.vector.quantize_mx(
-                        out=codes[:, g, cols].bitcast(FP8X4),
-                        scales=scales[:, g, cols],
-                        in_=grouped[:, g, cols, :].rearrange("p c t -> p (c t)"),
-                    )
+    for m in (FROM_X, FROM_H):
+        a_codes.append(acts.tile([P, PASSES, BATCH], U32, name="codes%d" % m, align_bytes=64))
+        a_scales.append(acts.tile([P, PASSES, BATCH], U8, name="scales%d" % m, align_bytes=64))
 
-        bias_cols_ps = prep_psum.tile([P, P], BF16)
-        nc.tensor.transpose(bias_cols_ps[:], bias_rows[:], ident_bf16[:])
-        bias_cols = consts.tile([P, 2, 3, UNIT_TILES], F32)
+    def transpose_rows(m, t):
+        grouped[m, t] = acts.tile([P, PASSES, P, PACK], BF16, name="grouped%d_%d" % (m, t), align_bytes=64)
+        row_words = a_rows[m][:, t, :].bitcast(F32)
+        flipped = psum.tile([P, PASSES, HALVES, P], F32, tag="bank")
+        for g in range(PASSES):
+            for u in range(HALVES):
+                nc.tensor.transpose(
+                    flipped[:, g, u, :],
+                    row_words[:, F32_PER_PASS * g + u : F32_PER_PASS * (g + 1) : HALVES],
+                    ident_f32[:],
+                )
+        grouped_words = (
+            grouped[m, t][:]
+            .rearrange("p g c t -> p (g c t)")
+            .bitcast(F32)
+            .rearrange("p (g c u) -> p g c u", g=PASSES, u=HALVES)
+        )
+        flipped_words = flipped[:].rearrange("p g u b -> p g b u")
+        if (m, t) in VECTOR_COPIES:
+            nc.vector.tensor_copy(out=grouped_words, in_=flipped_words)
+        else:
+            nc.scalar.copy(out=grouped_words, in_=flipped_words)
+
+    def quantise_rows(m, t):
+        cols = slice(t * P, (t + 1) * P)
+        for g in range(PASSES):
+            nc.vector.quantize_mx(
+                out=a_codes[m][:, g, cols].bitcast(FP8X4),
+                scales=a_scales[m][:, g, cols],
+                in_=grouped[m, t][:, g, :, :].rearrange("p c t -> p (c t)"),
+            )
+
+    bias_cols = consts.tile([P, 2, 3, UNIT_TILES], F32)
+    r_bias = consts.tile([P, UNIT_TILES], F32)
+    z_bias = consts.tile([P, UNITS], F32)
+
+    def add_z_biases(bank):
+        z_bias_ps = psum.tile([P, BANK], F32, tag="bank")
+        nc.tensor.matmul(z_bias_ps[:], lhsT=ones[:], rhs=z_bias_rows[:, bank * BANK : (bank + 1) * BANK], start=True, stop=True)
+        return z_bias_ps
+
+    def finish_z_biases(bank, z_bias_ps):
+        nc.vector.tensor_scalar(
+            out=z_bias[:, bank * BANK : (bank + 1) * BANK], in0=z_bias_ps[:], scalar1=0.2, scalar2=0.5, op0=ALU.mult, op1=ALU.add
+        )
+
+    def finish_unit_biases(bias_cols_ps):
         nc.vector.tensor_copy(
             out=bias_cols[:].rearrange("p b c j -> p (b c j)"), in_=bias_cols_ps[:, 0 : 2 * 3 * UNIT_TILES]
         )
-        r_bias = consts.tile([P, UNIT_TILES], F32)
         nc.vector.tensor_tensor(out=r_bias[:], in0=bias_cols[:, 0, GATE_R, :], in1=bias_cols[:, 1, GATE_R, :], op=ALU.add)
         nc.vector.tensor_scalar(out=r_bias[:], in0=r_bias[:], scalar1=0.2, scalar2=0.5, op0=ALU.mult, op1=ALU.add)
-        z_bias = consts.tile([P, UNITS], F32)
-        for bank in range(BANKS_PER_GATE):
-            z_bias_ps = prep_psum.tile([P, BANK], F32, bufs=2)
-            nc.tensor.matmul(z_bias_ps[:], lhsT=ones[:], rhs=z_bias_rows[:, bank * BANK : (bank + 1) * BANK], start=True, stop=True)
-            nc.vector.tensor_scalar(
-                out=z_bias[:, bank * BANK : (bank + 1) * BANK], in0=z_bias_ps[:], scalar1=0.2, scalar2=0.5, op0=ALU.mult, op1=ALU.add
-            )
+
+    tiles = [(m, t) for m in (FROM_X, FROM_H) for t in range(BATCH_TILES)]
+    for i in range(len(tiles)):
+        transpose_rows(*tiles[i])
+        if i >= 1:
+            quantise_rows(*tiles[i - 1])
+    z_bias_ps = [add_z_biases(bank) for bank in range(BANKS_PER_GATE)]
+    bias_cols_ps = psum.tile([P, P], BF16, tag="bank")
+    nc.tensor.transpose(bias_cols_ps[:], bias_rows[:], ident_bf16[:])
+    quantise_rows(*tiles[-1])
+    finish_z_biases(0, z_bias_ps[0])
 
     def weight_plane(m, g, first_col, cols):
         return w_planes[SCALE_ROWS * (PASSES * m + g) : P, first_col : first_col + cols]
@@ -185,49 +212,53 @@ def gru_cell(
     blocks = [(bank, t) for bank in range(BANKS_PER_GATE) for t in range(BATCH_TILES)]
     acc_z = {}
     z_relu = {}
-    with tc.psum_pool(name="z_psum", bufs=4, reuse_waits="tile") as z_psum:
 
-        def z_passes(i, m):
-            bank, t = blocks[i]
-            for g in range(PASSES):
-                nc.tensor.matmul_mx(
-                    out=acc_z[i][:],
-                    lhsT=a_codes[m][:, g, t * P : (t + 1) * P].bitcast(FP8X4),
-                    lhsT_scale=a_scales[m][:, g, t * P : (t + 1) * P],
-                    rhs=w_words[(m, GATE_Z, bank)][:, g, :].bitcast(FP8X4),
-                    rhs_scale=weight_plane(m, g, GATE_Z * UNITS + bank * BANK, BANK),
-                    start=((m, g) == both[0]),
-                    stop=((m, g) == both[-1]),
-                )
+    def z_passes(i, m):
+        bank, t = blocks[i]
+        for g in range(PASSES):
+            nc.tensor.matmul_mx(
+                out=acc_z[i][:],
+                lhsT=a_codes[m][:, g, t * P : (t + 1) * P].bitcast(FP8X4),
+                lhsT_scale=a_scales[m][:, g, t * P : (t + 1) * P],
+                rhs=w_words[(m, GATE_Z, bank)][:, g, :].bitcast(FP8X4),
+                rhs_scale=weight_plane(m, g, GATE_Z * UNITS + bank * BANK, BANK),
+                start=((m, g) == both[0]),
+                stop=((m, g) == both[-1]),
+            )
 
-        for i in range(len(blocks) + 1 + Z_LAG):
-            if i < len(blocks):
-                acc_z[i] = z_psum.tile([P, BANK], F32, name="acc_z")
-                z_passes(i, FROM_X)
-            if 1 <= i <= len(blocks):
-                bank, t = blocks[i - 1]
-                units = slice(bank * BANK, (bank + 1) * BANK)
-                z_passes(i - 1, FROM_H)
-                z_line = work.tile([P, BANK], F32)
-                nc.vector.scalar_tensor_tensor(
-                    out=z_line[:], in0=acc_z[i - 1][:], scalar=0.2, in1=z_bias[:, units], op0=ALU.mult, op1=ALU.add
-                )
-                z_relu[i - 1] = work.tile([P, BANK], F32, name="z_relu", bufs=Z_LAG + 1)
-                nc.scalar.activation(out=z_relu[i - 1][:], in_=z_line[:], func=ACT.Relu)
-                nc.scalar.activation(out=not_z[:, t, units], in_=z_line[:], func=ACT.Relu, bias=1.0, scale=-1.0)
-            if i > Z_LAG:
-                bank, t = blocks[i - 1 - Z_LAG]
-                units = slice(bank * BANK, (bank + 1) * BANK)
-                nc.vector.scalar_tensor_tensor(
-                    out=z_h[:, t, units],
-                    in0=z_relu[i - 1 - Z_LAG][:],
-                    scalar=1.0,
-                    in1=a_rows[FROM_H][:, t, units],
-                    op0=ALU.min,
-                    op1=ALU.mult,
-                )
+    for i in range(len(blocks) + X_LEAD + Z_LAG):
+        if i < len(blocks):
+            acc_z[i] = psum.tile([P, BANK], F32, name="acc_z", tag="bank")
+            z_passes(i, FROM_X)
+        done = i - X_LEAD
+        if 0 <= done < len(blocks):
+            bank, t = blocks[done]
+            units = slice(bank * BANK, (bank + 1) * BANK)
+            z_passes(done, FROM_H)
+            z_line = work.tile([P, BANK], F32)
+            nc.vector.scalar_tensor_tensor(
+                out=z_line[:], in0=acc_z[done][:], scalar=0.2, in1=z_bias[:, units], op0=ALU.mult, op1=ALU.add
+            )
+            z_relu[done] = work.tile([P, BANK], F32, name="z_relu", bufs=Z_LAG + 1)
+            nc.scalar.activation(out=z_relu[done][:], in_=z_line[:], func=ACT.Relu)
+            nc.scalar.activation(out=not_z[:, t, units], in_=z_line[:], func=ACT.Relu, bias=1.0, scale=-1.0)
+        if done == 0:
+            finish_z_biases(1, z_bias_ps[1])
+        if done == 1:
+            finish_unit_biases(bias_cols_ps)
+        late = done - Z_LAG
+        if late >= 0:
+            bank, t = blocks[late]
+            units = slice(bank * BANK, (bank + 1) * BANK)
+            nc.vector.scalar_tensor_tensor(
+                out=z_h[:, t, units],
+                in0=z_relu[late][:],
+                scalar=1.0,
+                in1=a_rows[FROM_H][:, t, units],
+                op0=ALU.min,
+                op1=ALU.mult,
+            )
 
-    psum = ctx.enter_context(tc.psum_pool(name="psum", bufs=2, reuse_waits="tile"))
     out_tiles = out.rearrange("(t b) n -> b t n", b=P)
 
     def units_by_batch(acc, gate, j, batch, passes):
@@ -253,15 +284,15 @@ def gru_cell(
             j, first, count = pieces[k]
             batch = slice(first * P, (first + count) * P)
             width = count * P
-            acc_r = psum.tile([P, BATCH], F32)
+            acc_r = psum.tile([P, BATCH], F32, tag="bank")
             units_by_batch(acc_r[:, :width], GATE_R, j, batch, both)
-            acc_rh = psum.tile([P, BATCH], F32)
+            acc_rh = psum.tile([P, BATCH], F32, tag="bank")
             units_by_batch(acc_rh[:, :width], GATE_H, j, batch, both[PASSES:])
-            acc_xh = psum.tile([P, BATCH], F32)
+            acc_xh = psum.tile([P, BATCH], F32, tag="bank")
             units_by_batch(acc_xh[:, :width], GATE_H, j, batch, both[:PASSES])
         if k >= 2:
             end_j, end_first, end_count = pieces[k - 2]
-            cand_t = psum.tile([P, BATCH_TILES, P], F32)
+            cand_t = psum.tile([P, BATCH_TILES, P], F32, tag="bank")
             for t in range(end_count):
                 nc.tensor.transpose(cand_t[:, t, :], cand[k - 2][:, t * P : (t + 1) * P], ident_f32[:])
 

@@ -32,6 +32,7 @@ SCALE_ROWS = 4
 VECTOR_COPIES = ((FROM_H, 1),)
 X_LEAD = 2
 Z_LAG = 2
+FLIP_RUNS = (1, 3, 5, 6, 7, 8)
 TAIL_TILES = 2
 
 FLOPS = 2 * 2 * BATCH * DEPTH * 3 * UNITS
@@ -95,7 +96,7 @@ def gru_cell(
     def load_rows(m, first, tiles):
         nc.sync.dma_start(
             out=a_rows[m][:, first : first + tiles, :],
-            in_=rows_dram[m][P * first : P * (first + tiles), :].rearrange("(t b) k -> b t k", b=P),
+            in_=rows_dram[m].rearrange("(b t) k -> b t k", t=BATCH_TILES)[:, first : first + tiles, :],
         )
 
     def load_words(m, gate, bank):
@@ -180,8 +181,8 @@ def gru_cell(
         return z_bias_ps
 
     def finish_z_biases(bank, z_bias_ps):
-        nc.vector.tensor_scalar(
-            out=z_bias[:, bank * BANK : (bank + 1) * BANK], in0=z_bias_ps[:], scalar1=0.2, scalar2=0.5, op0=ALU.mult, op1=ALU.add
+        nc.scalar.activation(
+            out=z_bias[:, bank * BANK : (bank + 1) * BANK], in_=z_bias_ps[:], func=ACT.Identity, bias=0.5, scale=0.2
         )
 
     def finish_unit_biases(bias_cols_ps):
@@ -200,7 +201,8 @@ def gru_cell(
     bias_cols_ps = psum.tile([P, P], BF16, tag="bank")
     nc.tensor.transpose(bias_cols_ps[:], bias_rows[:], ident_bf16[:])
     quantise_rows(*tiles[-1])
-    finish_z_biases(0, z_bias_ps[0])
+    for bank in range(BANKS_PER_GATE):
+        finish_z_biases(bank, z_bias_ps[bank])
 
     def weight_plane(m, g, first_col, cols):
         return w_planes[SCALE_ROWS * (PASSES * m + g) : P, first_col : first_col + cols]
@@ -242,8 +244,6 @@ def gru_cell(
             z_relu[done] = work.tile([P, BANK], F32, name="z_relu", bufs=Z_LAG + 1)
             nc.scalar.activation(out=z_relu[done][:], in_=z_line[:], func=ACT.Relu)
             nc.scalar.activation(out=not_z[:, t, units], in_=z_line[:], func=ACT.Relu, bias=1.0, scale=-1.0)
-        if done == 0:
-            finish_z_biases(1, z_bias_ps[1])
         if done == 1:
             finish_unit_biases(bias_cols_ps)
         late = done - Z_LAG
@@ -259,7 +259,7 @@ def gru_cell(
                 op1=ALU.mult,
             )
 
-    out_tiles = out.rearrange("(t b) n -> b t n", b=P)
+    out_tiles = out.rearrange("(b t) n -> b t n", t=BATCH_TILES)
 
     def units_by_batch(acc, gate, j, batch, passes):
         bank, inside = divmod(j, TILES_PER_BANK)
@@ -279,6 +279,9 @@ def gru_cell(
 
     pre_tanh = {}
     cand = {}
+    cand_t = {}
+    flipped_pieces = 0
+    ended_pieces = 0
     for k in range(len(pieces) + 2):
         if k < len(pieces):
             j, first, count = pieces[k]
@@ -290,11 +293,12 @@ def gru_cell(
             units_by_batch(acc_rh[:, :width], GATE_H, j, batch, both[PASSES:])
             acc_xh = psum.tile([P, BATCH], F32, tag="bank")
             units_by_batch(acc_xh[:, :width], GATE_H, j, batch, both[:PASSES])
-        if k >= 2:
-            end_j, end_first, end_count = pieces[k - 2]
-            cand_t = psum.tile([P, BATCH_TILES, P], F32, tag="bank")
-            for t in range(end_count):
-                nc.tensor.transpose(cand_t[:, t, :], cand[k - 2][:, t * P : (t + 1) * P], ident_f32[:])
+        if k - 2 in FLIP_RUNS:
+            for i in range(flipped_pieces, k - 1):
+                cand_t[i] = psum.tile([P, BATCH_TILES, P], F32, name="cand_t", tag="bank")
+                for t in range(pieces[i][2]):
+                    nc.tensor.transpose(cand_t[i][:, t, :], cand[i][:, t * P : (t + 1) * P], ident_f32[:])
+            flipped_pieces = k - 1
 
         if k < len(pieces):
             r_relu = work.tile([P, BATCH], F32)
@@ -306,7 +310,7 @@ def gru_cell(
         if 1 <= k <= len(pieces):
             tanh_j, tanh_first, tanh_count = pieces[k - 1]
             tanh_width = tanh_count * P
-            cand[k - 1] = work.tile([P, BATCH], F32, name="cand", bufs=3)
+            cand[k - 1] = work.tile([P, BATCH], F32, name="cand", bufs=4)
             nc.scalar.activation(
                 out=cand[k - 1][:, :tanh_width],
                 in_=pre_tanh[k - 1][:, :tanh_width],
@@ -315,22 +319,32 @@ def gru_cell(
                 scale=1.0,
             )
 
+        ending = list(range(ended_pieces, min(ended_pieces + 1, flipped_pieces) if k < len(pieces) else flipped_pieces))
+        ended_pieces += len(ending)
+        fresh = {}
         if k < len(pieces):
             gated = work.tile([P, BATCH], F32)
             nc.vector.scalar_tensor_tensor(
                 out=gated[:, :width], in0=r_relu[:, :width], scalar=1.0, in1=rec_h[:, :width], op0=ALU.min, op1=ALU.mult
             )
-        if k >= 2:
-            units = slice(end_j * P, (end_j + 1) * P)
-            tiles = slice(end_first, end_first + end_count)
-            fresh = work.tile([P, BATCH_TILES, P], F32)
+        for i in ending:
+            end_j, end_first, end_count = pieces[i]
+            fresh[i] = work.tile([P, BATCH_TILES, P], F32, name="fresh")
             nc.vector.scalar_tensor_tensor(
-                out=fresh[:, :end_count, :], in0=not_z[:, tiles, units], scalar=1.0, in1=cand_t[:, :end_count, :], op0=ALU.min, op1=ALU.mult
+                out=fresh[i][:, :end_count, :],
+                in0=not_z[:, end_first : end_first + end_count, end_j * P : (end_j + 1) * P],
+                scalar=1.0,
+                in1=cand_t[i][:, :end_count, :],
+                op0=ALU.min,
+                op1=ALU.mult,
             )
         if k < len(pieces):
             pre_tanh[k] = work.tile([P, BATCH], F32, name="pre_tanh")
             nc.vector.tensor_tensor(out=pre_tanh[k][:, :width], in0=acc_xh[:, :width], in1=gated[:, :width], op=ALU.add)
-        if k >= 2:
+        for i in ending:
+            end_j, end_first, end_count = pieces[i]
+            units = slice(end_j * P, (end_j + 1) * P)
+            tiles = slice(end_first, end_first + end_count)
             result = work.tile([P, BATCH_TILES, P], F32, bufs=3)
-            nc.vector.tensor_tensor(out=result[:, :end_count, :], in0=fresh[:, :end_count, :], in1=z_h[:, tiles, units], op=ALU.add)
+            nc.vector.tensor_tensor(out=result[:, :end_count, :], in0=fresh[i][:, :end_count, :], in1=z_h[:, tiles, units], op=ALU.add)
             nc.sync.dma_start(out=out_tiles[:, tiles, units], in_=result[:, :end_count, :])

@@ -30,7 +30,8 @@ BANKS_PER_GATE = UNITS // BANK
 TILES_PER_BANK = BANK // P
 SCALE_ROWS = 4
 VECTOR_COPIES = ((FROM_H, 1),)
-X_LEAD = 2
+X_LEAD = 1
+PROMPT_BLOCKS = 6
 Z_LAG = 2
 FLIP_RUNS = (1, 3, 5, 6, 7, 8)
 TAIL_TILES = 2
@@ -59,17 +60,19 @@ def gru_cell(
 
     ones = consts.tile([P, P], BF16)
     nc.vector.memset(ones[:], 1.0)
-    w_planes = consts.tile([P, 3 * UNITS], U8, align_bytes=64)
-    nc.vector.memset(w_planes[:, GATE_Z * UNITS : (GATE_Z + 1) * UNITS].bitcast(I32), 0)
+    w_planes = [consts.tile([P, 3 * UNITS], U8, name="w_planes%d" % m, align_bytes=64) for m in (FROM_X, FROM_H)]
+    nc.vector.memset(w_planes[FROM_X][:, GATE_Z * UNITS : (GATE_Z + 1) * UNITS].bitcast(I32), 0)
 
     bias_rows = consts.tile([P, P], BF16)
-    nc.vector.memset(bias_rows[:].bitcast(I32), 0)
     z_bias_rows = consts.tile([P, UNITS], BF16)
     nc.vector.memset(z_bias_rows[:].bitcast(I32), 0)
+    nc.vector.memset(bias_rows[:].bitcast(I32), 0)
+    nc.vector.memset(w_planes[FROM_H][:, GATE_Z * UNITS : (GATE_Z + 1) * UNITS].bitcast(I32), 0)
     unread = consts.tile([P, 1], F32)
     nc.scalar.activation(out=unread[:], in_=ones[:, 0:1], func=ACT.Tanh)
 
-    nc.vector.memset(w_planes[:, GATE_R * UNITS : (GATE_H + 1) * UNITS].bitcast(I32), 0)
+    for planes in w_planes:
+        nc.vector.memset(planes[:, GATE_R * UNITS : (GATE_H + 1) * UNITS].bitcast(I32), 0)
 
     ident_f32 = consts.tile([P, P], F32)
     make_identity(nc, ident_f32[:])
@@ -87,9 +90,9 @@ def gru_cell(
     def load_scales(m, first_gate, gates):
         cols = slice(first_gate * UNITS, (first_gate + gates) * UNITS)
         for quadrant in range(4):
-            first = 32 * quadrant + SCALE_ROWS * PASSES * m
+            first = 32 * quadrant
             nc.sync.dma_start(
-                out=w_planes[first : first + SCALE_ROWS * PASSES, cols].bitcast(I32),
+                out=w_planes[m][first : first + SCALE_ROWS * PASSES, cols].bitcast(I32),
                 in_=scales_dram[m][:, SCALE_ROWS * quadrant : SCALE_ROWS * (quadrant + 1), cols].bitcast(I32),
             )
 
@@ -118,8 +121,8 @@ def gru_cell(
     load_scales(FROM_X, GATE_Z, 1)
     load_rows(FROM_H, 2, 2)
     load_words(FROM_X, GATE_Z, 0)
-    load_scales(FROM_H, GATE_Z, 1)
     load_words(FROM_H, GATE_Z, 0)
+    load_scales(FROM_H, GATE_Z, 1)
     load_words(FROM_X, GATE_Z, 1)
     load_words(FROM_H, GATE_Z, 1)
     load_scales(FROM_X, GATE_R, 2)
@@ -197,15 +200,10 @@ def gru_cell(
         transpose_rows(*tiles[i])
         if i >= 1:
             quantise_rows(*tiles[i - 1])
-    z_bias_ps = [add_z_biases(bank) for bank in range(BANKS_PER_GATE)]
-    bias_cols_ps = psum.tile([P, P], BF16, tag="bank")
-    nc.tensor.transpose(bias_cols_ps[:], bias_rows[:], ident_bf16[:])
     quantise_rows(*tiles[-1])
-    for bank in range(BANKS_PER_GATE):
-        finish_z_biases(bank, z_bias_ps[bank])
 
     def weight_plane(m, g, first_col, cols):
-        return w_planes[SCALE_ROWS * (PASSES * m + g) : P, first_col : first_col + cols]
+        return w_planes[m][SCALE_ROWS * g : P, first_col : first_col + cols]
 
     both = [(m, g) for m in (FROM_X, FROM_H) for g in range(PASSES)]
 
@@ -228,7 +226,25 @@ def gru_cell(
                 stop=((m, g) == both[-1]),
             )
 
-    for i in range(len(blocks) + X_LEAD + Z_LAG):
+    z_line = {}
+
+    def relus(i):
+        bank, t = blocks[i]
+        z_relu[i] = work.tile([P, BANK], F32, name="z_relu", bufs=Z_LAG + 1)
+        nc.scalar.activation(out=z_relu[i][:], in_=z_line[i][:], func=ACT.Relu)
+        nc.scalar.activation(
+            out=not_z[:, t, bank * BANK : (bank + 1) * BANK], in_=z_line[i][:], func=ACT.Relu, bias=1.0, scale=-1.0
+        )
+
+    def multiply_by_h(i):
+        bank, t = blocks[i]
+        units = slice(bank * BANK, (bank + 1) * BANK)
+        nc.vector.scalar_tensor_tensor(
+            out=z_h[:, t, units], in0=z_relu[i][:], scalar=1.0, in1=a_rows[FROM_H][:, t, units], op0=ALU.min, op1=ALU.mult
+        )
+
+    finish_z_biases(0, add_z_biases(0))
+    for i in range(max(len(blocks) + X_LEAD, PROMPT_BLOCKS + X_LEAD + Z_LAG)):
         if i < len(blocks):
             acc_z[i] = psum.tile([P, BANK], F32, name="acc_z", tag="bank")
             z_passes(i, FROM_X)
@@ -237,27 +253,20 @@ def gru_cell(
             bank, t = blocks[done]
             units = slice(bank * BANK, (bank + 1) * BANK)
             z_passes(done, FROM_H)
-            z_line = work.tile([P, BANK], F32)
+            z_line[done] = work.tile([P, BANK], F32, name="z_line", bufs=4)
             nc.vector.scalar_tensor_tensor(
-                out=z_line[:], in0=acc_z[done][:], scalar=0.2, in1=z_bias[:, units], op0=ALU.mult, op1=ALU.add
+                out=z_line[done][:], in0=acc_z[done][:], scalar=0.2, in1=z_bias[:, units], op0=ALU.mult, op1=ALU.add
             )
-            z_relu[done] = work.tile([P, BANK], F32, name="z_relu", bufs=Z_LAG + 1)
-            nc.scalar.activation(out=z_relu[done][:], in_=z_line[:], func=ACT.Relu)
-            nc.scalar.activation(out=not_z[:, t, units], in_=z_line[:], func=ACT.Relu, bias=1.0, scale=-1.0)
+            if done < PROMPT_BLOCKS:
+                relus(done)
         if done == 1:
+            finish_z_biases(1, add_z_biases(1))
+            bias_cols_ps = psum.tile([P, P], BF16, tag="bank")
+            nc.tensor.transpose(bias_cols_ps[:], bias_rows[:], ident_bf16[:])
             finish_unit_biases(bias_cols_ps)
         late = done - Z_LAG
-        if late >= 0:
-            bank, t = blocks[late]
-            units = slice(bank * BANK, (bank + 1) * BANK)
-            nc.vector.scalar_tensor_tensor(
-                out=z_h[:, t, units],
-                in0=z_relu[late][:],
-                scalar=1.0,
-                in1=a_rows[FROM_H][:, t, units],
-                op0=ALU.min,
-                op1=ALU.mult,
-            )
+        if 0 <= late < PROMPT_BLOCKS:
+            multiply_by_h(late)
 
     out_tiles = out.rearrange("(b t) n -> b t n", t=BATCH_TILES)
 
@@ -287,10 +296,11 @@ def gru_cell(
             j, first, count = pieces[k]
             batch = slice(first * P, (first + count) * P)
             width = count * P
-            acc_r = psum.tile([P, BATCH], F32, tag="bank")
-            units_by_batch(acc_r[:, :width], GATE_R, j, batch, both)
-            acc_rh = psum.tile([P, BATCH], F32, tag="bank")
-            units_by_batch(acc_rh[:, :width], GATE_H, j, batch, both[PASSES:])
+            if first == 0:
+                acc_r = psum.tile([P, BATCH], F32, tag="bank")
+                units_by_batch(acc_r[:], GATE_R, j, slice(0, BATCH), both)
+                acc_rh = psum.tile([P, BATCH], F32, tag="bank")
+                units_by_batch(acc_rh[:], GATE_H, j, slice(0, BATCH), both[PASSES:])
             acc_xh = psum.tile([P, BATCH], F32, tag="bank")
             units_by_batch(acc_xh[:, :width], GATE_H, j, batch, both[:PASSES])
         if k - 2 in FLIP_RUNS:
@@ -302,11 +312,14 @@ def gru_cell(
 
         if k < len(pieces):
             r_relu = work.tile([P, BATCH], F32)
-            nc.scalar.activation(out=r_relu[:, :width], in_=acc_r[:, :width], func=ACT.Relu, bias=r_bias[:, j : j + 1], scale=0.2)
+            nc.scalar.activation(out=r_relu[:, :width], in_=acc_r[:, batch], func=ACT.Relu, bias=r_bias[:, j : j + 1], scale=0.2)
             rec_h = work.tile([P, BATCH], F32)
             nc.scalar.activation(
-                out=rec_h[:, :width], in_=acc_rh[:, :width], func=ACT.Identity, bias=bias_cols[:, 1, GATE_H, j : j + 1], scale=1.0
+                out=rec_h[:, :width], in_=acc_rh[:, batch], func=ACT.Identity, bias=bias_cols[:, 1, GATE_H, j : j + 1], scale=1.0
             )
+        waiting_block = PROMPT_BLOCKS + k
+        if waiting_block < len(blocks):
+            relus(waiting_block)
         if 1 <= k <= len(pieces):
             tanh_j, tanh_first, tanh_count = pieces[k - 1]
             tanh_width = tanh_count * P
@@ -348,3 +361,5 @@ def gru_cell(
             result = work.tile([P, BATCH_TILES, P], F32, bufs=3)
             nc.vector.tensor_tensor(out=result[:, :end_count, :], in0=fresh[i][:, :end_count, :], in1=z_h[:, tiles, units], op=ALU.add)
             nc.sync.dma_start(out=out_tiles[:, tiles, units], in_=result[:, :end_count, :])
+        if waiting_block < len(blocks):
+            multiply_by_h(waiting_block)

@@ -60,19 +60,20 @@ def gru_cell(
 
     ones = consts.tile([P, P], BF16)
     nc.vector.memset(ones[:], 1.0)
-    w_planes = [consts.tile([P, 3 * UNITS], U8, name="w_planes%d" % m, align_bytes=64) for m in (FROM_X, FROM_H)]
-    nc.vector.memset(w_planes[FROM_X][:, GATE_Z * UNITS : (GATE_Z + 1) * UNITS].bitcast(I32), 0)
+    z_planes = [consts.tile([P, UNITS], U8, name="z_planes%d" % m, align_bytes=64) for m in (FROM_X, FROM_H)]
+    nc.vector.memset(z_planes[FROM_X][:].bitcast(I32), 0)
 
     bias_rows = consts.tile([P, P], BF16)
     z_bias_rows = consts.tile([P, UNITS], BF16)
     nc.vector.memset(z_bias_rows[:].bitcast(I32), 0)
     nc.vector.memset(bias_rows[:].bitcast(I32), 0)
-    nc.vector.memset(w_planes[FROM_H][:, GATE_Z * UNITS : (GATE_Z + 1) * UNITS].bitcast(I32), 0)
+    nc.vector.memset(z_planes[FROM_H][:].bitcast(I32), 0)
     unread = consts.tile([P, 1], F32)
     nc.scalar.activation(out=unread[:], in_=ones[:, 0:1], func=ACT.Tanh)
 
-    for planes in w_planes:
-        nc.vector.memset(planes[:, GATE_R * UNITS : (GATE_H + 1) * UNITS].bitcast(I32), 0)
+    rh_planes = [consts.tile([P, PASSES, BANK], U8, name="rh_planes%d" % m, align_bytes=64) for m in (FROM_X, FROM_H)]
+    for planes in rh_planes:
+        nc.vector.memset(planes[:].rearrange("p g c -> p (g c)").bitcast(I32), 0)
 
     ident_f32 = consts.tile([P, P], F32)
     make_identity(nc, ident_f32[:])
@@ -87,13 +88,22 @@ def gru_cell(
     a_rows = [acts.tile([P, BATCH_TILES, DEPTH], BF16, name="rows%d" % m) for m in (FROM_X, FROM_H)]
     w_words = {}
 
-    def load_scales(m, first_gate, gates):
-        cols = slice(first_gate * UNITS, (first_gate + gates) * UNITS)
+    def load_z_scales(m):
         for quadrant in range(4):
             first = 32 * quadrant
             nc.sync.dma_start(
-                out=w_planes[m][first : first + SCALE_ROWS * PASSES, cols].bitcast(I32),
-                in_=scales_dram[m][:, SCALE_ROWS * quadrant : SCALE_ROWS * (quadrant + 1), cols].bitcast(I32),
+                out=z_planes[m][first : first + SCALE_ROWS * PASSES, :].bitcast(I32),
+                in_=scales_dram[m][:, SCALE_ROWS * quadrant : SCALE_ROWS * (quadrant + 1), :UNITS].bitcast(I32),
+            )
+
+    def load_rh_scales(m, g):
+        for quadrant in range(4):
+            first = 32 * quadrant
+            nc.sync.dma_start(
+                out=rh_planes[m][first : first + SCALE_ROWS * 2 * BANKS_PER_GATE, g, :].bitcast(I32),
+                in_=scales_dram[m][g, SCALE_ROWS * quadrant : SCALE_ROWS * (quadrant + 1), UNITS:]
+                .bitcast(I32)
+                .rearrange("r (b c) -> b r c", b=2 * BANKS_PER_GATE),
             )
 
     def load_rows(m, first, tiles):
@@ -118,20 +128,25 @@ def gru_cell(
     load_rows(FROM_X, 1, 1)
     load_rows(FROM_X, 2, 2)
     load_rows(FROM_H, 0, 2)
-    load_scales(FROM_X, GATE_Z, 1)
+    load_z_scales(FROM_X)
     load_rows(FROM_H, 2, 2)
     load_words(FROM_X, GATE_Z, 0)
     load_words(FROM_H, GATE_Z, 0)
-    load_scales(FROM_H, GATE_Z, 1)
+    load_z_scales(FROM_H)
     load_words(FROM_X, GATE_Z, 1)
+    load_rh_scales(FROM_X, 0)
     load_words(FROM_H, GATE_Z, 1)
-    load_scales(FROM_X, GATE_R, 2)
-    load_scales(FROM_H, GATE_R, 2)
-    for bank in range(BANKS_PER_GATE):
-        load_words(FROM_X, GATE_R, bank)
-        load_words(FROM_H, GATE_R, bank)
-        load_words(FROM_H, GATE_H, bank)
-        load_words(FROM_X, GATE_H, bank)
+    load_rh_scales(FROM_X, 1)
+    load_words(FROM_X, GATE_R, 0)
+    load_rh_scales(FROM_H, 0)
+    load_words(FROM_H, GATE_R, 0)
+    load_rh_scales(FROM_H, 1)
+    load_words(FROM_H, GATE_H, 0)
+    load_words(FROM_X, GATE_H, 0)
+    load_words(FROM_X, GATE_R, 1)
+    load_words(FROM_H, GATE_R, 1)
+    load_words(FROM_H, GATE_H, 1)
+    load_words(FROM_X, GATE_H, 1)
 
     psum = ctx.enter_context(tc.psum_pool(name="psum", bufs=8))
 
@@ -202,8 +217,10 @@ def gru_cell(
             quantise_rows(*tiles[i - 1])
     quantise_rows(*tiles[-1])
 
-    def weight_plane(m, g, first_col, cols):
-        return w_planes[m][SCALE_ROWS * g : P, first_col : first_col + cols]
+    def rh_plane(m, g, gate, j):
+        bank, inside = divmod(j, TILES_PER_BANK)
+        block = BANKS_PER_GATE * (gate - GATE_R) + bank
+        return rh_planes[m][SCALE_ROWS * block : P, g, inside * P : (inside + 1) * P]
 
     both = [(m, g) for m in (FROM_X, FROM_H) for g in range(PASSES)]
 
@@ -221,7 +238,7 @@ def gru_cell(
                 lhsT=a_codes[m][:, g, t * P : (t + 1) * P].bitcast(FP8X4),
                 lhsT_scale=a_scales[m][:, g, t * P : (t + 1) * P],
                 rhs=w_words[(m, GATE_Z, bank)][:, g, :].bitcast(FP8X4),
-                rhs_scale=weight_plane(m, g, GATE_Z * UNITS + bank * BANK, BANK),
+                rhs_scale=z_planes[m][SCALE_ROWS * g : P, bank * BANK : (bank + 1) * BANK],
                 start=((m, g) == both[0]),
                 stop=((m, g) == both[-1]),
             )
@@ -276,7 +293,7 @@ def gru_cell(
             nc.tensor.matmul_mx(
                 out=acc,
                 lhsT=w_words[(m, gate, bank)][:, g, inside * P : (inside + 1) * P].bitcast(FP8X4),
-                lhsT_scale=weight_plane(m, g, gate * UNITS + j * P, P),
+                lhsT_scale=rh_plane(m, g, gate, j),
                 rhs=a_codes[m][:, g, batch].bitcast(FP8X4),
                 rhs_scale=a_scales[m][:, g, batch],
                 start=((m, g) == passes[0]),

@@ -30,9 +30,10 @@ BANKS_PER_GATE = UNITS // BANK
 TILES_PER_BANK = BANK // P
 SCALE_ROWS = 4
 VECTOR_COPIES = ((FROM_H, 1),)
-X_LEAD = 1
+X_LEAD = 3
 PROMPT_BLOCKS = 6
 Z_LAG = 2
+EARLY_R = 2
 FLIP_RUNS = (1, 3, 5, 6, 7, 8)
 TAIL_TILES = 2
 
@@ -303,6 +304,8 @@ def gru_cell(
     pieces = [(j, 0, BATCH_TILES) for j in range(UNIT_TILES - 1)]
     pieces.extend([(UNIT_TILES - 1, first, TAIL_TILES) for first in range(0, BATCH_TILES, TAIL_TILES)])
 
+    acc_r = {}
+    r_tiles = 0
     pre_tanh = {}
     cand = {}
     cand_t = {}
@@ -314,8 +317,10 @@ def gru_cell(
             batch = slice(first * P, (first + count) * P)
             width = count * P
             if first == 0:
-                acc_r = psum.tile([P, BATCH], F32, tag="bank")
-                units_by_batch(acc_r[:], GATE_R, j, slice(0, BATCH), both)
+                while r_tiles < (EARLY_R if j == 0 else j + 1):
+                    acc_r[r_tiles] = psum.tile([P, BATCH], F32, name="acc_r", tag="bank")
+                    units_by_batch(acc_r[r_tiles][:], GATE_R, r_tiles, slice(0, BATCH), both)
+                    r_tiles += 1
                 acc_rh = psum.tile([P, BATCH], F32, tag="bank")
                 units_by_batch(acc_rh[:], GATE_H, j, slice(0, BATCH), both[PASSES:])
             acc_xh = psum.tile([P, BATCH], F32, tag="bank")
@@ -329,7 +334,7 @@ def gru_cell(
 
         if k < len(pieces):
             r_relu = work.tile([P, BATCH], F32)
-            nc.scalar.activation(out=r_relu[:, :width], in_=acc_r[:, batch], func=ACT.Relu, bias=r_bias[:, j : j + 1], scale=0.2)
+            nc.scalar.activation(out=r_relu[:, :width], in_=acc_r[j][:, batch], func=ACT.Relu, bias=r_bias[:, j : j + 1], scale=0.2)
             rec_h = work.tile([P, BATCH], F32)
             nc.scalar.activation(
                 out=rec_h[:, :width], in_=acc_rh[:, batch], func=ACT.Identity, bias=bias_cols[:, 1, GATE_H, j : j + 1], scale=1.0

from contextlib import ExitStack

import concourse.mybir as mybir
from concourse.masks import make_identity

F32 = mybir.dt.float32
BF16 = mybir.dt.bfloat16
I32 = mybir.dt.int32
U32 = mybir.dt.uint32
U8 = mybir.dt.uint8
FP8X4 = mybir.dt.float8_e4m3fn_x4
ACT = mybir.ActivationFunctionType
ALU = mybir.AluOpType

P = 128
PACK = 4
K_PASS = P * PACK
BATCH = 512
DEPTH = 1024
UNITS = 1024
PASSES = DEPTH // K_PASS
BATCH_TILES = BATCH // P
UNIT_TILES = UNITS // P
GATE_Z, GATE_R, GATE_H = 0, 1, 2
FROM_X, FROM_H = 0, 1
HALVES = 2
F32_PER_PASS = K_PASS // 2
BANK = 512
BANKS_PER_GATE = UNITS // BANK
TILES_PER_BANK = BANK // P
SCALE_ROWS = 4
VECTOR_COPIES = ((FROM_H, 1),)
X_LEAD = 3
PROMPT_BLOCKS = 6
Z_LAG = 2
EARLY_R = 2
FLIP_RUNS = (1, 3, 5, 6, 7, 8)
TAIL_TILES = 2

FLOPS = 2 * 2 * BATCH * DEPTH * 3 * UNITS


def tile_gruskipcell_kernel(
    tc, inputs, h_tm1, kernel_words, kernel_scales, recurrent_kernel_words, recurrent_kernel_scales, bias, out
):
    with ExitStack() as ctx:
        gru_cell(
            ctx, tc, inputs, h_tm1, kernel_words, kernel_scales, recurrent_kernel_words, recurrent_kernel_scales, bias, out
        )


def gru_cell(
    ctx, tc, inputs, h_tm1, kernel_words, kernel_scales, recurrent_kernel_words, recurrent_kernel_scales, bias, out
):
    nc = tc.nc
    ctx.enter_context(tc.manual_schedule())
    consts = ctx.enter_context(tc.tile_pool(name="consts", bufs=1))
    acts = ctx.enter_context(tc.tile_pool(name="acts", bufs=1))
    weights = ctx.enter_context(tc.tile_pool(name="weights", bufs=1))
    work = ctx.enter_context(tc.tile_pool(name="work", bufs=2))

    ones = consts.tile([P, P], BF16)
    nc.vector.memset(ones[:], 1.0)
    z_planes = [consts.tile([P, UNITS], U8, name="z_planes%d" % m, align_bytes=64) for m in (FROM_X, FROM_H)]
    nc.vector.memset(z_planes[FROM_X][:].bitcast(I32), 0)

    bias_rows = consts.tile([P, P], BF16)
    z_bias_rows = consts.tile([P, UNITS], BF16)
    nc.vector.memset(z_bias_rows[:].bitcast(I32), 0)
    nc.vector.memset(bias_rows[:].bitcast(I32), 0)
    nc.vector.memset(z_planes[FROM_H][:].bitcast(I32), 0)
    unread = consts.tile([P, 1], F32)
    nc.scalar.activation(out=unread[:], in_=ones[:, 0:1], func=ACT.Tanh)

    rh_planes = [consts.tile([P, PASSES, BANK], U8, name="rh_planes%d" % m, align_bytes=64) for m in (FROM_X, FROM_H)]
    for planes in rh_planes:
        nc.vector.memset(planes[:].rearrange("p g c -> p (g c)").bitcast(I32), 0)

    ident_f32 = consts.tile([P, P], F32)
    make_identity(nc, ident_f32[:])
    nc.gpsimd.dma_start(out=z_bias_rows[0:2, :], in_=bias[:, GATE_Z * UNITS : (GATE_Z + 1) * UNITS])
    nc.gpsimd.dma_start(out=bias_rows[0 : 2 * 3 * UNIT_TILES, :], in_=bias.rearrange("b (c n) -> (b c) n", n=P))
    ident_bf16 = consts.tile([P, P], BF16)
    make_identity(nc, ident_bf16[:])

    rows_dram = (inputs, h_tm1)
    scales_dram = (kernel_scales, recurrent_kernel_scales)
    words_dram = (kernel_words, recurrent_kernel_words)
    a_rows = [acts.tile([P, BATCH_TILES, DEPTH], BF16, name="rows%d" % m) for m in (FROM_X, FROM_H)]
    w_words = {}

    def load_z_scales(m):
        for quadrant in range(4):
            first = 32 * quadrant
            nc.sync.dma_start(
                out=z_planes[m][first : first + SCALE_ROWS * PASSES, :].bitcast(I32),
                in_=scales_dram[m][:, SCALE_ROWS * quadrant : SCALE_ROWS * (quadrant + 1), :UNITS].bitcast(I32),
            )

    def load_rh_scales(m, g):
        for quadrant in range(4):
            first = 32 * quadrant
            nc.sync.dma_start(
                out=rh_planes[m][first : first + SCALE_ROWS * 2 * BANKS_PER_GATE, g, :].bitcast(I32),
                in_=scales_dram[m][g, SCALE_ROWS * quadrant : SCALE_ROWS * (quadrant + 1), UNITS:]
                .bitcast(I32)
                .rearrange("r (b c) -> b r c", b=2 * BANKS_PER_GATE),
            )

    def load_rows(m, first, tiles):
        nc.sync.dma_start(
            out=a_rows[m][:, first : first + tiles, :],
            in_=rows_dram[m].rearrange("(b t) k -> b t k", t=BATCH_TILES)[:, first : first + tiles, :],
        )

    def load_words(m, gate, bank):
        words = weights.tile([P, PASSES, BANK], U32, name="w%d_%d_%d" % (m, gate, bank), align_bytes=64)
        w_words[(m, gate, bank)] = words
        first = gate * UNITS + bank * BANK
        nc.sync.dma_start(
            out=words[:].bitcast(I32),
            in_=words_dram[m]
            .rearrange("g p n t -> g p (n t)")
            .bitcast(I32)[:, :, first : first + BANK]
            .rearrange("g p n -> p g n"),
        )

    load_rows(FROM_X, 0, 1)
    load_rows(FROM_X, 1, 1)
    load_rows(FROM_X, 2, 2)
    load_rows(FROM_H, 0, 2)
    load_z_scales(FROM_X)
    load_rows(FROM_H, 2, 2)
    load_words(FROM_X, GATE_Z, 0)
    load_words(FROM_H, GATE_Z, 0)
    load_z_scales(FROM_H)
    load_words(FROM_X, GATE_Z, 1)
    load_rh_scales(FROM_X, 0)
    load_words(FROM_H, GATE_Z, 1)
    load_rh_scales(FROM_X, 1)
    load_words(FROM_X, GATE_R, 0)
    load_rh_scales(FROM_H, 0)
    load_words(FROM_H, GATE_R, 0)
    load_rh_scales(FROM_H, 1)
    load_words(FROM_H, GATE_H, 0)
    load_words(FROM_X, GATE_H, 0)
    load_words(FROM_X, GATE_R, 1)
    load_words(FROM_H, GATE_R, 1)
    load_words(FROM_H, GATE_H, 1)
    load_words(FROM_X, GATE_H, 1)

    psum = ctx.enter_context(tc.psum_pool(name="psum", bufs=8))

    grouped = {}
    a_codes = []
    a_scales = []
    for m in (FROM_X, FROM_H):
        a_codes.append(acts.tile([P, PASSES, BATCH], U32, name="codes%d" % m, align_bytes=64))
        a_scales.append(acts.tile([P, PASSES, BATCH], U8, name="scales%d" % m, align_bytes=64))

    def transpose_rows(m, t):
        grouped[m, t] = acts.tile([P, PASSES, P, PACK], BF16, name="grouped%d_%d" % (m, t), align_bytes=64)
        row_words = a_rows[m][:, t, :].bitcast(F32)
        flipped = psum.tile([P, PASSES, HALVES, P], F32, tag="bank")
        for g in range(PASSES):
            for u in range(HALVES):
                nc.tensor.transpose(
                    flipped[:, g, u, :],
                    row_words[:, F32_PER_PASS * g + u : F32_PER_PASS * (g + 1) : HALVES],
                    ident_f32[:],
                )
        grouped_words = (
            grouped[m, t][:]
            .rearrange("p g c t -> p (g c t)")
            .bitcast(F32)
            .rearrange("p (g c u) -> p g c u", g=PASSES, u=HALVES)
        )
        flipped_words = flipped[:].rearrange("p g u b -> p g b u")
        if (m, t) in VECTOR_COPIES:
            nc.vector.tensor_copy(out=grouped_words, in_=flipped_words)
        else:
            nc.scalar.copy(out=grouped_words, in_=flipped_words)

    def quantise_rows(m, t):
        cols = slice(t * P, (t + 1) * P)
        for g in range(PASSES):
            nc.vector.quantize_mx(
                out=a_codes[m][:, g, cols].bitcast(FP8X4),
                scales=a_scales[m][:, g, cols],
                in_=grouped[m, t][:, g, :, :].rearrange("p c t -> p (c t)"),
            )

    bias_cols = consts.tile([P, 2, 3, UNIT_TILES], F32)
    r_bias = consts.tile([P, UNIT_TILES], F32)
    z_bias = consts.tile([P, UNITS], F32)

    def add_z_biases(bank):
        z_bias_ps = psum.tile([P, BANK], F32, tag="bank")
        nc.tensor.matmul(z_bias_ps[:], lhsT=ones[:], rhs=z_bias_rows[:, bank * BANK : (bank + 1) * BANK], start=True, stop=True)
        return z_bias_ps

    def finish_z_biases(bank, z_bias_ps):
        nc.scalar.activation(
            out=z_bias[:, bank * BANK : (bank + 1) * BANK], in_=z_bias_ps[:], func=ACT.Identity, bias=0.5, scale=0.2
        )

    def finish_unit_biases(bias_cols_ps):
        nc.vector.tensor_copy(
            out=bias_cols[:].rearrange("p b c j -> p (b c j)"), in_=bias_cols_ps[:, 0 : 2 * 3 * UNIT_TILES]
        )
        nc.vector.tensor_tensor(out=r_bias[:], in0=bias_cols[:, 0, GATE_R, :], in1=bias_cols[:, 1, GATE_R, :], op=ALU.add)
        nc.vector.tensor_scalar(out=r_bias[:], in0=r_bias[:], scalar1=0.2, scalar2=0.5, op0=ALU.mult, op1=ALU.add)

    tiles = [(m, t) for m in (FROM_X, FROM_H) for t in range(BATCH_TILES)]
    for i in range(len(tiles)):
        transpose_rows(*tiles[i])
        if i >= 1:
            quantise_rows(*tiles[i - 1])
    quantise_rows(*tiles[-1])

    def rh_plane(m, g, gate, j):
        bank, inside = divmod(j, TILES_PER_BANK)
        block = BANKS_PER_GATE * (gate - GATE_R) + bank
        return rh_planes[m][SCALE_ROWS * block : P, g, inside * P : (inside + 1) * P]

    both = [(m, g) for m in (FROM_X, FROM_H) for g in range(PASSES)]

    z_h = acts.tile([P, BATCH_TILES, UNITS], F32)
    not_z = acts.tile([P, BATCH_TILES, UNITS], F32)
    blocks = [(bank, t) for bank in range(BANKS_PER_GATE) for t in range(BATCH_TILES)]
    acc_z = {}
    z_relu = {}

    def z_passes(i, m):
        bank, t = blocks[i]
        for g in range(PASSES):
            nc.tensor.matmul_mx(
                out=acc_z[i][:],
                lhsT=a_codes[m][:, g, t * P : (t + 1) * P].bitcast(FP8X4),
                lhsT_scale=a_scales[m][:, g, t * P : (t + 1) * P],
                rhs=w_words[(m, GATE_Z, bank)][:, g, :].bitcast(FP8X4),
                rhs_scale=z_planes[m][SCALE_ROWS * g : P, bank * BANK : (bank + 1) * BANK],
                start=((m, g) == both[0]),
                stop=((m, g) == both[-1]),
            )

    z_line = {}

    def relus(i):
        bank, t = blocks[i]
        z_relu[i] = work.tile([P, BANK], F32, name="z_relu", bufs=Z_LAG + 1)
        nc.scalar.activation(out=z_relu[i][:], in_=z_line[i][:], func=ACT.Relu)
        nc.scalar.activation(
            out=not_z[:, t, bank * BANK : (bank + 1) * BANK], in_=z_line[i][:], func=ACT.Relu, bias=1.0, scale=-1.0
        )

    def multiply_by_h(i):
        bank, t = blocks[i]
        units = slice(bank * BANK, (bank + 1) * BANK)
        nc.vector.scalar_tensor_tensor(
            out=z_h[:, t, units], in0=z_relu[i][:], scalar=1.0, in1=a_rows[FROM_H][:, t, units], op0=ALU.min, op1=ALU.mult
        )

    finish_z_biases(0, add_z_biases(0))
    for i in range(max(len(blocks) + X_LEAD, PROMPT_BLOCKS + X_LEAD + Z_LAG)):
        if i < len(blocks):
            acc_z[i] = psum.tile([P, BANK], F32, name="acc_z", tag="bank")
            z_passes(i, FROM_X)
        done = i - X_LEAD
        if 0 <= done < len(blocks):
            bank, t = blocks[done]
            units = slice(bank * BANK, (bank + 1) * BANK)
            z_passes(done, FROM_H)
            z_line[done] = work.tile([P, BANK], F32, name="z_line", bufs=4)
            nc.vector.scalar_tensor_tensor(
                out=z_line[done][:], in0=acc_z[done][:], scalar=0.2, in1=z_bias[:, units], op0=ALU.mult, op1=ALU.add
            )
            if done < PROMPT_BLOCKS:
                relus(done)
        if done == 1:
            finish_z_biases(1, add_z_biases(1))
            bias_cols_ps = psum.tile([P, P], BF16, tag="bank")
            nc.tensor.transpose(bias_cols_ps[:], bias_rows[:], ident_bf16[:])
            finish_unit_biases(bias_cols_ps)
        late = done - Z_LAG
        if 0 <= late < PROMPT_BLOCKS:
            multiply_by_h(late)

    out_tiles = out.rearrange("(b t) n -> b t n", t=BATCH_TILES)

    def units_by_batch(acc, gate, j, batch, passes):
        bank, inside = divmod(j, TILES_PER_BANK)
        for m, g in passes:
            nc.tensor.matmul_mx(
                out=acc,
                lhsT=w_words[(m, gate, bank)][:, g, inside * P : (inside + 1) * P].bitcast(FP8X4),
                lhsT_scale=rh_plane(m, g, gate, j),
                rhs=a_codes[m][:, g, batch].bitcast(FP8X4),
                rhs_scale=a_scales[m][:, g, batch],
                start=((m, g) == passes[0]),
                stop=((m, g) == passes[-1]),
            )

    pieces = [(j, 0, BATCH_TILES) for j in range(UNIT_TILES - 1)]
    pieces.extend([(UNIT_TILES - 1, first, TAIL_TILES) for first in range(0, BATCH_TILES, TAIL_TILES)])

    acc_r = {}
    r_tiles = 0
    pre_tanh = {}
    cand = {}
    cand_t = {}
    flipped_pieces = 0
    ended_pieces = 0
    for k in range(len(pieces) + 2):
        if k < len(pieces):
            j, first, count = pieces[k]
            batch = slice(first * P, (first + count) * P)
            width = count * P
            if first == 0:
                while r_tiles < (EARLY_R if j == 0 else j + 1):
                    acc_r[r_tiles] = psum.tile([P, BATCH], F32, name="acc_r", tag="bank")
                    units_by_batch(acc_r[r_tiles][:], GATE_R, r_tiles, slice(0, BATCH), both)
                    r_tiles += 1
                acc_rh = psum.tile([P, BATCH], F32, tag="bank")
                units_by_batch(acc_rh[:], GATE_H, j, slice(0, BATCH), both[PASSES:])
            acc_xh = psum.tile([P, BATCH], F32, tag="bank")
            units_by_batch(acc_xh[:, :width], GATE_H, j, batch, both[:PASSES])
        if k - 2 in FLIP_RUNS:
            for i in range(flipped_pieces, k - 1):
                cand_t[i] = psum.tile([P, BATCH_TILES, P], F32, name="cand_t", tag="bank")
                for t in range(pieces[i][2]):
                    nc.tensor.transpose(cand_t[i][:, t, :], cand[i][:, t * P : (t + 1) * P], ident_f32[:])
            flipped_pieces = k - 1

        if k < len(pieces):
            r_relu = work.tile([P, BATCH], F32)
            nc.scalar.activation(out=r_relu[:, :width], in_=acc_r[j][:, batch], func=ACT.Relu, bias=r_bias[:, j : j + 1], scale=0.2)
            rec_h = work.tile([P, BATCH], F32)
            nc.scalar.activation(
                out=rec_h[:, :width], in_=acc_rh[:, batch], func=ACT.Identity, bias=bias_cols[:, 1, GATE_H, j : j + 1], scale=1.0
            )
        waiting_block = PROMPT_BLOCKS + k
        if waiting_block < len(blocks):
            relus(waiting_block)
        if 1 <= k <= len(pieces):
            tanh_j, tanh_first, tanh_count = pieces[k - 1]
            tanh_width = tanh_count * P
            cand[k - 1] = work.tile([P, BATCH], F32, name="cand", bufs=4)
            nc.scalar.activation(
                out=cand[k - 1][:, :tanh_width],
                in_=pre_tanh[k - 1][:, :tanh_width],
                func=ACT.Tanh,
                bias=bias_cols[:, 0, GATE_H, tanh_j : tanh_j + 1],
                scale=1.0,
            )

        ending = list(range(ended_pieces, min(ended_pieces + 1, flipped_pieces) if k < len(pieces) else flipped_pieces))
        ended_pieces += len(ending)
        fresh = {}
        if k < len(pieces):
            gated = work.tile([P, BATCH], F32)
            nc.vector.scalar_tensor_tensor(
                out=gated[:, :width], in0=r_relu[:, :width], scalar=1.0, in1=rec_h[:, :width], op0=ALU.min, op1=ALU.mult
            )
        for i in ending:
            end_j, end_first, end_count = pieces[i]
            fresh[i] = work.tile([P, BATCH_TILES, P], F32, name="fresh")
            nc.vector.scalar_tensor_tensor(
                out=fresh[i][:, :end_count, :],
                in0=not_z[:, end_first : end_first + end_count, end_j * P : (end_j + 1) * P],
                scalar=1.0,
                in1=cand_t[i][:, :end_count, :],
                op0=ALU.min,
                op1=ALU.mult,
            )
        if k < len(pieces):
            pre_tanh[k] = work.tile([P, BATCH], F32, name="pre_tanh")
            nc.vector.tensor_tensor(out=pre_tanh[k][:, :width], in0=acc_xh[:, :width], in1=gated[:, :width], op=ALU.add)
        for i in ending:
            end_j, end_first, end_count = pieces[i]
            units = slice(end_j * P, (end_j + 1) * P)
            tiles = slice(end_first, end_first + end_count)
            result = work.tile([P, BATCH_TILES, P], F32, bufs=3)
            nc.vector.tensor_tensor(out=result[:, :end_count, :], in0=fresh[i][:, :end_count, :], in1=z_h[:, tiles, units], op=ALU.add)
            nc.sync.dma_start(out=out_tiles[:, tiles, units], in_=result[:, :end_count, :])
        if waiting_block < len(blocks):
            multiply_by_h(waiting_block)
